import numpy as np
import ml_dtypes


def mxq(x, axis, fmt="e4m3"):
    dtype, down = {"e4m3": (ml_dtypes.float8_e4m3fn, 7), "e5m2": (ml_dtypes.float8_e5m2, 14)}[fmt]
    v = np.moveaxis(np.asarray(x, np.float32).astype(ml_dtypes.bfloat16).astype(np.float64), axis, -1)
    blocks = v.reshape(v.shape[:-1] + (-1, 32))
    amax = np.abs(blocks).max(-1, keepdims=True)
    byte = np.maximum(np.where(amax > 0, np.frexp(amax)[1] - 1 + 127, 0) - down, 1)
    scale = np.exp2(byte - 127.0)
    codes = (blocks / scale).astype(np.float32).astype(dtype).astype(np.float64)
    return np.moveaxis((codes * scale).reshape(v.shape), -1, axis)


WIDE = False


def mx_kscale(k):
    if not WIDE:
        return np.ones(k)
    levels = np.array([10, -10, 5, -5, 0])
    if k % 512:
        return np.exp2(np.random.permutation(np.resize(levels, k // 32))).repeat(32)
    a = np.empty((k // 512, 16))
    for p in range(k // 512):
        a[p, :8] = np.random.permutation(np.resize(levels, 8))
        for g in range(8):
            far = levels[np.abs(levels - a[p, g]) >= 10]
            a[p, g + 8] = far[np.random.randint(len(far))]
    return np.exp2(a.ravel()).repeat(32)


BF16 = ml_dtypes.bfloat16


def bf(x):
    return np.asarray(x, np.float32).astype(BF16)


def f64(x):
    return np.asarray(x).astype(np.float64)


B, S, D, N, A, F = 32, 64, 512, 128, 128, 1024
LN_EPS = 1e-5


def setup_inputs():
    t = mx_kscale(F)
    return {
        "actions": bf(np.random.standard_normal((B, N, A))),
        "W_ae": bf(np.random.standard_normal((F, A)) / np.sqrt(A)),
        "b_ae": bf(np.random.standard_normal(F) * 0.4),
        "ln_g": bf((1.0 + 0.1 * np.random.standard_normal(F)) * t),
        "ln_b": bf(0.2 * np.random.standard_normal(F) * t),
        "Wv": bf(np.random.standard_normal((F, F)) / np.sqrt(F) / t[None, :]),
    }


def reference(actions, W_ae, b_ae, ln_g, ln_b, Wv):
    a = f64(actions) @ f64(W_ae).T + f64(b_ae)
    mu = a.mean(-1, keepdims=True)
    var = ((a - mu) ** 2).mean(-1, keepdims=True)
    a_n = (a - mu) / np.sqrt(var + LN_EPS) * f64(ln_g) + f64(ln_b)
    a_n = a_n
    return mxq(a_n, 2, "e4m3") @ mxq(f64(Wv), 1, "e4m3").T

@@ -1,0 +1,356 @@
+from contextlib import ExitStack
+
+import concourse.mybir as mybir
+from concourse.masks import make_identity
+
+F32 = mybir.dt.float32
+BF16 = mybir.dt.bfloat16
+U32 = mybir.dt.uint32
+U8 = mybir.dt.uint8
+FP8X4 = mybir.dt.float8_e4m3fn_x4
+ALU = mybir.AluOpType
+ACT = mybir.ActivationFunctionType
+AXIS = mybir.AxisListType
+
+P = 128
+TOKENS = 32 * 128
+A = 128
+F = 1024
+LN_EPS = 1e-5
+
+TILES = TOKENS // P
+GROUP = 4
+GROUPS = TILES // GROUP
+GROUP_TOKENS = GROUP * P
+CHUNKS = F // P
+PACK = 4
+PASSES = F // (P * PACK)
+BANK = 512
+HALVES = F // BANK
+X_PITCH = A + 32
+STAT_COLS = A + 2
+
+STATS_LEAD = 6
+TRANSPOSE_LAG = GROUP
+REGROUP_LAG = TRANSPOSE_LAG + 2
+PROJECT_LAG = TRANSPOSE_LAG + GROUP + 3
+
+FLOPS = 2 * TOKENS * A * F + 2 * TOKENS * F * F
+
+
+def tile_actionbindingattention_pa_t_kernel(tc, actions, W_ae, b_ae, ln_g, ln_b, Wv, out):
+    nc = tc.nc
+    x_dram = actions.rearrange("b n a -> (b n) a").rearrange("(p i) a -> p i a", i=TILES)
+    out_dram = out.rearrange("b n o -> (b n) o").rearrange("(p i) o -> p i o", i=TILES)
+
+    with ExitStack() as ctx:
+        ctx.enter_context(tc.manual_schedule())
+        const = ctx.enter_context(tc.tile_pool(name="const", bufs=1))
+        stat_pool = ctx.enter_context(tc.tile_pool(name="stat_pool", bufs=3))
+        bias_pool = ctx.enter_context(tc.tile_pool(name="bias_pool", bufs=6))
+        n_pool = ctx.enter_context(tc.tile_pool(name="n_pool", bufs=3 * GROUP))
+        work = ctx.enter_context(tc.tile_pool(name="work", bufs=2))
+        o_pool = ctx.enter_context(tc.tile_pool(name="o_pool", bufs=4))
+        psum_y = ctx.enter_context(tc.psum_pool(name="psum_y", bufs=2))
+        psum_a = ctx.enter_context(tc.psum_pool(name="psum_a", bufs=2))
+        psum_t = ctx.enter_context(tc.psum_pool(name="psum_t", bufs=2))
+        psum_o = ctx.enter_context(tc.psum_pool(name="psum_o", bufs=2))
+
+        w_nat = const.tile([P, CHUNKS, A], BF16)
+        nc.sync.dma_start(
+            out=w_nat[:].rearrange("p (g t) a -> p g (t a)", g=PASSES),
+            in_=W_ae.rearrange("(g p t) a -> p g (t a)", g=PASSES, t=PACK),
+        )
+        g_bf = const.tile([P, PASSES, PACK], BF16)
+        s_bf = const.tile([P, PASSES, PACK], BF16)
+        b_bf = const.tile([P, PASSES, PACK], BF16)
+        for cols_bf, vec in ((b_bf, b_ae), (g_bf, ln_g), (s_bf, ln_b)):
+            nc.sync.dma_start(out=cols_bf[:], in_=vec.rearrange("(g p t) -> p g t", g=PASSES, t=PACK))
+        x_aug = const.tile([P, TILES, X_PITCH], BF16)
+        nc.vector.memset(x_aug[:, :, A : A + 1], 2.0)
+        x_piece = TILES // 4
+        for q in range(4):
+            tiles_q = slice(q * x_piece, (q + 1) * x_piece)
+            nc.sync.dma_start(out=x_aug[:, tiles_q, 0:A], in_=x_dram[:, tiles_q, :])
+        wv_nat = const.tile([P, CHUNKS, F], BF16)
+        wv_dram = Wv.rearrange("(oc p) k -> p oc k", p=P)
+        for q in range(4):
+            nc.sync.dma_start(out=wv_nat[:, 2 * q : 2 * q + 2, :], in_=wv_dram[:, 2 * q : 2 * q + 2, :])
+
+        ident_bf = const.tile([P, P], BF16)
+        make_identity(nc, ident_bf[:])
+        ident_f32 = const.tile([P, P], F32)
+        make_identity(nc, ident_f32[:])
+        b_row = const.tile([P, F], BF16)
+        nc.gpsimd.dma_start(out=b_row[:], in_=b_ae.partition_broadcast(P))
+        b_bc = const.tile([P, F], BF16)
+        neg_mean_bf = const.tile([P, P], BF16)
+        nc.vector.memset(neg_mean_bf[:], -1.0 / F)
+        neg_mean_f32 = const.tile([P, P], F32)
+        nc.vector.memset(neg_mean_f32[:], -1.0 / F)
+
+        xT = const.tile([P, TILES, P], BF16)
+
+        def transpose_actions(q):
+            xT_ps = psum_a.tile([P, CHUNKS, P], BF16, tag="a")
+            for r in range(CHUNKS):
+                nc.tensor.transpose(xT_ps[:, r, :], x_aug[:, q * CHUNKS + r, 0:A], ident_bf[:])
+            nc.scalar.copy(out=xT[:, q * CHUNKS : (q + 1) * CHUNKS, :], in_=xT_ps[:])
+
+        wT_ps = psum_t.tile([P, CHUNKS, P], BF16, tag="t")
+        for c in range(CHUNKS):
+            nc.tensor.transpose(wT_ps[:, c, :], w_nat[:, c, :], ident_bf[:])
+        wT = const.tile([P, F], BF16)
+        nc.scalar.copy(out=wT[:], in_=wT_ps[:].rearrange("p c f -> p (c f)"))
+        vec_cols = const.tile([P, 3 * CHUNKS], F32)
+        for v, cols_bf in enumerate((g_bf, s_bf, b_bf)):
+            nc.vector.tensor_copy(
+                out=vec_cols[:, v * CHUNKS : (v + 1) * CHUNKS], in_=cols_bf[:].rearrange("p g t -> p (g t)")
+            )
+        gain = vec_cols[:, 0:CHUNKS]
+        shift_f = vec_cols[:, CHUNKS : 2 * CHUNKS]
+        b_cols = vec_cols[:, 2 * CHUNKS : 3 * CHUNKS]
+
+        neg_wbar_ps = psum_y.tile([P, A], F32, tag="y")
+        for c in range(CHUNKS):
+            nc.tensor.matmul(
+                out=neg_wbar_ps[:], lhsT=neg_mean_bf[:], rhs=w_nat[:, c, :], start=(c == 0), stop=(c == CHUNKS - 1)
+            )
+        neg_b_ps = psum_y.tile([P, CHUNKS], F32, tag="y")
+        nc.tensor.matmul(out=neg_b_ps[:], lhsT=neg_mean_f32[:], rhs=b_cols, start=True, stop=True)
+        for q in range(TILES // CHUNKS):
+            transpose_actions(q)
+        neg_bbar = const.tile([P, 1], F32)
+        nc.vector.tensor_reduce(out=neg_bbar[:], in_=neg_b_ps[:], axis=AXIS.X, op=ALU.add)
+        centred = const.tile([P, CHUNKS, A + 1], F32)
+        nc.vector.tensor_tensor(
+            out=centred[:, :, 0:A],
+            in0=w_nat[:],
+            in1=neg_wbar_ps[:].unsqueeze(1).to_broadcast([P, CHUNKS, A]),
+            op=ALU.add,
+        )
+        nc.vector.tensor_scalar(
+            out=centred[:, :, A], in0=b_cols, scalar1=neg_bbar[:], scalar2=None, op0=ALU.add
+        )
+        bc_sq = const.tile([P, CHUNKS], F32)
+        nc.vector.tensor_tensor(out=bc_sq[:], in0=centred[:, :, A], in1=centred[:, :, A], op=ALU.mult)
+        gram_ps = psum_y.tile([P, STAT_COLS], F32, tag="y")
+        for c in range(CHUNKS):
+            nc.tensor.matmul(
+                out=gram_ps[:, 0 : A + 1],
+                lhsT=centred[:, c, 0:A],
+                rhs=centred[:, c, :],
+                start=(c == 0),
+                stop=(c == CHUNKS - 1),
+            )
+        for c in range(CHUNKS):
+            nc.tensor.matmul(
+                out=gram_ps[:, A + 1 : A + 2],
+                lhsT=w_nat[:, c, :],
+                rhs=neg_mean_bf[:, 0:1],
+                start=(c == 0),
+                stop=(c == CHUNKS - 1),
+            )
+        neg_c0_ps = psum_y.tile([P, CHUNKS], F32, tag="y")
+        nc.tensor.matmul(out=neg_c0_ps[:], lhsT=neg_mean_f32[:], rhs=bc_sq[:], start=True, stop=True)
+        nc.vector.tensor_copy(
+            out=b_bc[:].rearrange("p (g t m) -> p g t m", g=PASSES, t=PACK),
+            in_=b_row[:].rearrange("p (g m t) -> p g t m", g=PASSES, t=PACK),
+        )
+        stat_hi = const.tile([P, STAT_COLS], BF16)
+        nc.vector.tensor_copy(out=stat_hi[:], in_=gram_ps[:])
+        stat_lo = const.tile([P, STAT_COLS], BF16)
+        nc.vector.tensor_tensor(out=stat_lo[:], in0=gram_ps[:], in1=stat_hi[:], op=ALU.subtract)
+        neg_var_b = const.tile([P, 1], F32)
+        nc.vector.tensor_reduce(out=neg_var_b[:], in_=neg_c0_ps[:], axis=AXIS.X, op=ALU.add)
+        var_bias = const.tile([P, 1], F32)
+        nc.vector.tensor_scalar(
+            out=var_bias[:], in0=neg_var_b[:], scalar1=-1.0, scalar2=LN_EPS, op0=ALU.mult, op1=ALU.add
+        )
+
+        wv_grouped = const.tile([P, PASSES, F, PACK], BF16, align_bytes=64)
+        wv_codes = const.tile([P, PASSES, F], U32, align_bytes=64)
+        wv_scales = const.tile([P, PASSES, F], U8, align_bytes=64)
+
+        def prepare_wv(oc):
+            wvT_ps = psum_o.tile([P, CHUNKS, P], BF16, tag="o")
+            for kc in range(CHUNKS):
+                g, t = divmod(kc, PACK)
+                k_first = g * PACK * P + t
+                nc.tensor.transpose(
+                    wvT_ps[:, kc, :], wv_nat[:, oc, k_first : (g + 1) * PACK * P : PACK], ident_bf[:]
+                )
+            for g in range(PASSES):
+                nc.scalar.copy(
+                    out=wv_grouped[:, g, oc * P : (oc + 1) * P, :],
+                    in_=wvT_ps[:, g * PACK : (g + 1) * PACK, :].rearrange("p j o -> p o j"),
+                )
+            if (oc + 1) * P % BANK == 0:
+                cols = slice((oc + 1) * P - BANK, (oc + 1) * P)
+                for g in range(PASSES):
+                    nc.vector.quantize_mx(
+                        out=wv_codes[:, g, cols].bitcast(FP8X4),
+                        scales=wv_scales[:, g, cols],
+                        in_=wv_grouped[:, g, cols, :].rearrange("p o j -> p (o j)"),
+                    )
+
+        stat_ps = {}
+        f_var = {}
+        rstd = {}
+        bias_rows = {}
+        n_tiles = {}
+        planes = {}
+        grouped = {}
+        quantised = {}
+
+        def statistics(pair):
+            group = pair * 2 // GROUP
+            if pair * 2 % GROUP == 0:
+                f_var_tile = stat_pool.tile([P, GROUP], F32)
+                f_var[group] = f_var_tile
+            y_ps = psum_y.tile([P, 2, STAT_COLS], F32, tag="y")
+            stat_ps[pair] = y_ps
+            for e in range(2):
+                nc.tensor.matmul(out=y_ps[:, e, :], lhsT=xT[:, 2 * pair + e, :], rhs=stat_hi[:], start=True, stop=False)
+                nc.tensor.matmul(out=y_ps[:, e, :], lhsT=xT[:, 2 * pair + e, :], rhs=stat_lo[:], start=False, stop=True)
+            for e in range(2):
+                tile_i = 2 * pair + e
+                products = work.tile([P, A + 1], F32)
+                nc.vector.scalar_tensor_tensor(
+                    out=products[:],
+                    in0=y_ps[:, e, 0 : A + 1],
+                    scalar=1.0,
+                    in1=x_aug[:, tile_i, 0 : A + 1],
+                    op0=ALU.mult,
+                    op1=ALU.mult,
+                    accum_out=f_var[group][:, tile_i % GROUP : tile_i % GROUP + 1],
+                )
+
+        def finish_statistics(group):
+            std = stat_pool.tile([P, GROUP], F32)
+            nc.scalar.activation(out=std[:], in_=f_var[group][:], func=ACT.Sqrt, bias=var_bias[:], scale=1.0 / F)
+            rstd_tile = stat_pool.tile([P, GROUP], F32)
+            rstd[group] = rstd_tile
+            nc.vector.reciprocal(out=rstd_tile[:], in_=std[:])
+            shift_t = stat_pool.tile([P, GROUP], F32)
+            for e in range(GROUP // 2):
+                nc.vector.scalar_tensor_tensor(
+                    out=shift_t[:, 2 * e : 2 * e + 2],
+                    in0=stat_ps[group * GROUP // 2 + e][:, :, A + 1],
+                    scalar=neg_bbar[:],
+                    in1=rstd_tile[:, 2 * e : 2 * e + 2],
+                    op0=ALU.add,
+                    op1=ALU.mult,
+                )
+            for r in range(GROUP):
+                bias_tile = bias_pool.tile([P, F], F32)
+                bias_rows[group * GROUP + r] = bias_tile
+                for h in range(HALVES):
+                    cols = slice(h * BANK, (h + 1) * BANK)
+                    nc.gpsimd.tensor_scalar(
+                        out=bias_tile[:, cols],
+                        in0=b_bc[:, cols],
+                        scalar1=rstd_tile[:, r : r + 1],
+                        scalar2=shift_t[:, r : r + 1],
+                        op0=ALU.mult,
+                        op1=ALU.add,
+                    )
+
+        def encode(tile_i):
+            n_sb = n_pool.tile([P, F], F32)
+            n_tiles[tile_i] = n_sb
+            for h in range(HALVES):
+                cols = slice(h * BANK, (h + 1) * BANK)
+                a_ps = psum_a.tile([P, BANK], F32, tag="a")
+                nc.tensor.matmul(out=a_ps[:], lhsT=xT[:, tile_i, :], rhs=wT[:, cols], start=True, stop=True)
+                nc.vector.scalar_tensor_tensor(
+                    out=n_sb[:, cols],
+                    in0=a_ps[:],
+                    scalar=rstd[tile_i // GROUP][:, tile_i % GROUP : tile_i % GROUP + 1],
+                    in1=bias_rows[tile_i][:, cols],
+                    op0=ALU.mult,
+                    op1=ALU.add,
+                )
+
+        def transpose_chunks(group, first, count):
+            if first == 0:
+                planes_tile = work.tile([P, CHUNKS, GROUP_TOKENS], BF16)
+                planes[group] = planes_tile
+            for c in range(first, first + count):
+                t_ps = psum_t.tile([P, GROUP_TOKENS], F32, tag="t")
+                for r in range(GROUP):
+                    nc.tensor.transpose(
+                        t_ps[:, r * P : (r + 1) * P], n_tiles[group * GROUP + r][:, c * P : (c + 1) * P], ident_f32[:]
+                    )
+                nc.scalar.activation(
+                    out=planes[group][:, c, :],
+                    in_=t_ps[:],
+                    func=ACT.Identity,
+                    scale=gain[:, c : c + 1],
+                    bias=shift_f[:, c : c + 1],
+                )
+
+        def regroup(group, g):
+            grouped_tile = work.tile([P, GROUP_TOKENS, PACK], BF16, align_bytes=64, bufs=3)
+            grouped[(group, g)] = grouped_tile
+            nc.vector.tensor_copy(
+                out=grouped_tile[:].rearrange("p (c i) j -> p c j i", i=4),
+                in_=planes[group][:, g * PACK : (g + 1) * PACK, :].rearrange("p j (c i) -> p c j i", i=4),
+            )
+
+        def quantise(group, g):
+            if g == 0:
+                codes_tile = work.tile([P, PASSES, GROUP_TOKENS], U32, align_bytes=64)
+                scales_tile = work.tile([P, PASSES, GROUP_TOKENS], U8, align_bytes=64)
+                quantised[group] = (codes_tile, scales_tile)
+            codes, scales = quantised[group]
+            nc.vector.quantize_mx(
+                out=codes[:, g, :].bitcast(FP8X4),
+                scales=scales[:, g, :],
+                in_=grouped[(group, g)][:].rearrange("p w j -> p (w j)"),
+            )
+
+        def project(tile_i):
+            codes, scales = quantised[tile_i // GROUP]
+            tokens = slice(tile_i % GROUP * P, (tile_i % GROUP + 1) * P)
+            o_sb = o_pool.tile([P, F], F32)
+            for h in range(HALVES):
+                cols = slice(h * BANK, (h + 1) * BANK)
+                o_ps = psum_o.tile([P, BANK], F32, tag="o")
+                for g in range(PASSES):
+                    nc.tensor.matmul_mx(
+                        out=o_ps[:],
+                        lhsT=codes[:, g, tokens].bitcast(FP8X4),
+                        lhsT_scale=scales[:, g, tokens],
+                        rhs=wv_codes[:, g, cols].bitcast(FP8X4),
+                        rhs_scale=wv_scales[:, g, cols],
+                        start=(g == 0),
+                        stop=(g == PASSES - 1),
+                    )
+                if tile_i + PROJECT_LAG >= TILES and h == 1:
+                    nc.vector.tensor_copy(out=o_sb[:, cols], in_=o_ps[:])
+                else:
+                    nc.scalar.copy(out=o_sb[:, cols], in_=o_ps[:])
+            nc.sync.dma_start(out=out_dram[:, tile_i, :], in_=o_sb[:])
+
+        chunks_a_slot = CHUNKS // GROUP
+        for slot in range(-STATS_LEAD, TILES + PROJECT_LAG):
+            if 0 <= slot - PROJECT_LAG:
+                project(slot - PROJECT_LAG)
+            if 0 <= slot < TILES:
+                encode(slot)
+            ahead = slot + STATS_LEAD
+            if ahead < TILES and ahead % 2 == 0:
+                statistics(ahead // 2)
+            if ahead < TILES and ahead % GROUP == GROUP - 1:
+                finish_statistics(ahead // GROUP)
+            if 0 <= slot < CHUNKS:
+                prepare_wv(slot)
+            behind = slot - TRANSPOSE_LAG
+            if 0 <= behind < TILES:
+                transpose_chunks(behind // GROUP, behind % GROUP * chunks_a_slot, chunks_a_slot)
+            behind = slot - REGROUP_LAG
+            if 0 <= behind < TILES and behind % 2 == 0:
+                regroup(behind // GROUP, behind % GROUP // 2)
+            if 0 <= behind < TILES and behind % 2 == 1:
+                quantise(behind // GROUP, behind % GROUP // 2)

@@ -19,8 +19,7 @@ F = 1024
 LN_EPS = 1e-5
 
 TILES = TOKENS // P
-GROUP = 4
-GROUPS = TILES // GROUP
+GROUP = 2
 GROUP_TOKENS = GROUP * P
 CHUNKS = F // P
 PACK = 4
@@ -32,8 +31,9 @@ STAT_COLS = A + 2
 
 STATS_LEAD = 6
 TRANSPOSE_LAG = GROUP
-REGROUP_LAG = TRANSPOSE_LAG + 2
-PROJECT_LAG = TRANSPOSE_LAG + GROUP + 3
+REGROUP_LAG = TRANSPOSE_LAG + 1
+QUANTISE_LAG = REGROUP_LAG + 1
+PROJECT_LAG = QUANTISE_LAG + 3
 
 FLOPS = 2 * TOKENS * A * F + 2 * TOKENS * F * F
 
@@ -46,10 +46,10 @@ def tile_actionbindingattention_pa_t_kernel(tc, actions, W_ae, b_ae, ln_g, ln_b,
     with ExitStack() as ctx:
         ctx.enter_context(tc.manual_schedule())
         const = ctx.enter_context(tc.tile_pool(name="const", bufs=1))
-        stat_pool = ctx.enter_context(tc.tile_pool(name="stat_pool", bufs=3))
-        bias_pool = ctx.enter_context(tc.tile_pool(name="bias_pool", bufs=6))
-        n_pool = ctx.enter_context(tc.tile_pool(name="n_pool", bufs=3 * GROUP))
-        work = ctx.enter_context(tc.tile_pool(name="work", bufs=2))
+        stat_pool = ctx.enter_context(tc.tile_pool(name="stat_pool", bufs=STATS_LEAD // GROUP + 2))
+        bias_pool = ctx.enter_context(tc.tile_pool(name="bias_pool", bufs=STATS_LEAD + 2))
+        n_pool = ctx.enter_context(tc.tile_pool(name="n_pool", bufs=8))
+        work = ctx.enter_context(tc.tile_pool(name="work", bufs=3))
         o_pool = ctx.enter_context(tc.tile_pool(name="o_pool", bufs=4))
         psum_y = ctx.enter_context(tc.psum_pool(name="psum_y", bufs=2))
         psum_a = ctx.enter_context(tc.psum_pool(name="psum_a", bufs=2))
@@ -64,85 +64,47 @@ def tile_actionbindingattention_pa_t_kernel(tc, actions, W_ae, b_ae, ln_g, ln_b,
         g_bf = const.tile([P, PASSES, PACK], BF16)
         s_bf = const.tile([P, PASSES, PACK], BF16)
         b_bf = const.tile([P, PASSES, PACK], BF16)
-        for cols_bf, vec in ((b_bf, b_ae), (g_bf, ln_g), (s_bf, ln_b)):
-            nc.sync.dma_start(out=cols_bf[:], in_=vec.rearrange("(g p t) -> p g t", g=PASSES, t=PACK))
+        nc.sync.dma_start(out=b_bf[:], in_=b_ae.rearrange("(g p t) -> p g t", g=PASSES, t=PACK))
         x_aug = const.tile([P, TILES, X_PITCH], BF16)
-        nc.vector.memset(x_aug[:, :, A : A + 1], 2.0)
         x_piece = TILES // 4
-        for q in range(4):
+
+        def load_actions(q):
             tiles_q = slice(q * x_piece, (q + 1) * x_piece)
             nc.sync.dma_start(out=x_aug[:, tiles_q, 0:A], in_=x_dram[:, tiles_q, :])
+
+        load_actions(0)
+        for cols_bf, vec in ((g_bf, ln_g), (s_bf, ln_b)):
+            nc.sync.dma_start(out=cols_bf[:], in_=vec.rearrange("(g p t) -> p g t", g=PASSES, t=PACK))
+        load_actions(1)
         wv_nat = const.tile([P, CHUNKS, F], BF16)
         wv_dram = Wv.rearrange("(oc p) k -> p oc k", p=P)
         for q in range(4):
             nc.sync.dma_start(out=wv_nat[:, 2 * q : 2 * q + 2, :], in_=wv_dram[:, 2 * q : 2 * q + 2, :])
+            if q in (1, 2):
+                load_actions(q + 1)
 
-        ident_bf = const.tile([P, P], BF16)
-        make_identity(nc, ident_bf[:])
-        ident_f32 = const.tile([P, P], F32)
-        make_identity(nc, ident_f32[:])
-        b_row = const.tile([P, F], BF16)
-        nc.gpsimd.dma_start(out=b_row[:], in_=b_ae.partition_broadcast(P))
-        b_bc = const.tile([P, F], BF16)
         neg_mean_bf = const.tile([P, P], BF16)
         nc.vector.memset(neg_mean_bf[:], -1.0 / F)
         neg_mean_f32 = const.tile([P, P], F32)
         nc.vector.memset(neg_mean_f32[:], -1.0 / F)
-
-        xT = const.tile([P, TILES, P], BF16)
-
-        def transpose_actions(q):
-            xT_ps = psum_a.tile([P, CHUNKS, P], BF16, tag="a")
-            for r in range(CHUNKS):
-                nc.tensor.transpose(xT_ps[:, r, :], x_aug[:, q * CHUNKS + r, 0:A], ident_bf[:])
-            nc.scalar.copy(out=xT[:, q * CHUNKS : (q + 1) * CHUNKS, :], in_=xT_ps[:])
-
-        wT_ps = psum_t.tile([P, CHUNKS, P], BF16, tag="t")
-        for c in range(CHUNKS):
-            nc.tensor.transpose(wT_ps[:, c, :], w_nat[:, c, :], ident_bf[:])
-        wT = const.tile([P, F], BF16)
-        nc.scalar.copy(out=wT[:], in_=wT_ps[:].rearrange("p c f -> p (c f)"))
-        vec_cols = const.tile([P, 3 * CHUNKS], F32)
-        for v, cols_bf in enumerate((g_bf, s_bf, b_bf)):
-            nc.vector.tensor_copy(
-                out=vec_cols[:, v * CHUNKS : (v + 1) * CHUNKS], in_=cols_bf[:].rearrange("p g t -> p (g t)")
-            )
-        gain = vec_cols[:, 0:CHUNKS]
-        shift_f = vec_cols[:, CHUNKS : 2 * CHUNKS]
-        b_cols = vec_cols[:, 2 * CHUNKS : 3 * CHUNKS]
+        ident_bf = const.tile([P, P], BF16)
+        make_identity(nc, ident_bf[:])
+        ident_f32 = const.tile([P, P], F32)
+        make_identity(nc, ident_f32[:])
+        neg_half = const.tile([P, GROUP], F32)
+        nc.gpsimd.memset(neg_half[:], -0.5)
+        nc.vector.memset(x_aug[:, :, A : A + 1], 2.0)
 
         neg_wbar_ps = psum_y.tile([P, A], F32, tag="y")
         for c in range(CHUNKS):
             nc.tensor.matmul(
                 out=neg_wbar_ps[:], lhsT=neg_mean_bf[:], rhs=w_nat[:, c, :], start=(c == 0), stop=(c == CHUNKS - 1)
             )
+        b_cols = const.tile([P, CHUNKS], F32)
+        nc.vector.tensor_copy(out=b_cols[:], in_=b_bf[:].rearrange("p g t -> p (g t)"))
         neg_b_ps = psum_y.tile([P, CHUNKS], F32, tag="y")
-        nc.tensor.matmul(out=neg_b_ps[:], lhsT=neg_mean_f32[:], rhs=b_cols, start=True, stop=True)
-        for q in range(TILES // CHUNKS):
-            transpose_actions(q)
-        neg_bbar = const.tile([P, 1], F32)
-        nc.vector.tensor_reduce(out=neg_bbar[:], in_=neg_b_ps[:], axis=AXIS.X, op=ALU.add)
-        centred = const.tile([P, CHUNKS, A + 1], F32)
-        nc.vector.tensor_tensor(
-            out=centred[:, :, 0:A],
-            in0=w_nat[:],
-            in1=neg_wbar_ps[:].unsqueeze(1).to_broadcast([P, CHUNKS, A]),
-            op=ALU.add,
-        )
-        nc.vector.tensor_scalar(
-            out=centred[:, :, A], in0=b_cols, scalar1=neg_bbar[:], scalar2=None, op0=ALU.add
-        )
-        bc_sq = const.tile([P, CHUNKS], F32)
-        nc.vector.tensor_tensor(out=bc_sq[:], in0=centred[:, :, A], in1=centred[:, :, A], op=ALU.mult)
-        gram_ps = psum_y.tile([P, STAT_COLS], F32, tag="y")
-        for c in range(CHUNKS):
-            nc.tensor.matmul(
-                out=gram_ps[:, 0 : A + 1],
-                lhsT=centred[:, c, 0:A],
-                rhs=centred[:, c, :],
-                start=(c == 0),
-                stop=(c == CHUNKS - 1),
-            )
+        nc.tensor.matmul(out=neg_b_ps[:], lhsT=neg_mean_f32[:], rhs=b_cols[:], start=True, stop=True)
+        gram_ps = psum_a.tile([P, STAT_COLS], F32, tag="a")
         for c in range(CHUNKS):
             nc.tensor.matmul(
                 out=gram_ps[:, A + 1 : A + 2],
@@ -151,12 +113,53 @@ def tile_actionbindingattention_pa_t_kernel(tc, actions, W_ae, b_ae, ln_g, ln_b,
                 start=(c == 0),
                 stop=(c == CHUNKS - 1),
             )
-        neg_c0_ps = psum_y.tile([P, CHUNKS], F32, tag="y")
+        xT = const.tile([P, TILES, P], BF16)
+
+        def transpose_actions(q):
+            xT_ps = psum_o.tile([P, CHUNKS, P], BF16, tag="o")
+            for r in range(CHUNKS):
+                nc.tensor.transpose(xT_ps[:, r, :], x_aug[:, q * CHUNKS + r, 0:A], ident_bf[:])
+            nc.scalar.copy(out=xT[:, q * CHUNKS : (q + 1) * CHUNKS, :], in_=xT_ps[:])
+
+        transpose_actions(0)
+        centred = const.tile([P, CHUNKS, A + 1], F32)
+        for half in range(2):
+            chunks = slice(half * CHUNKS // 2, (half + 1) * CHUNKS // 2)
+            nc.vector.tensor_tensor(
+                out=centred[:, chunks, 0:A],
+                in0=w_nat[:, chunks, :],
+                in1=neg_wbar_ps[:].unsqueeze(1).to_broadcast([P, CHUNKS // 2, A]),
+                op=ALU.add,
+            )
+            if half == 0:
+                neg_bbar = const.tile([P, 1], F32)
+                nc.vector.tensor_reduce(out=neg_bbar[:], in_=neg_b_ps[:], axis=AXIS.X, op=ALU.add)
+                nc.vector.tensor_scalar(
+                    out=centred[:, :, A], in0=b_cols[:], scalar1=neg_bbar[:], scalar2=None, op0=ALU.add
+                )
+        bc_sq = const.tile([P, CHUNKS], F32)
+        nc.vector.tensor_tensor(out=bc_sq[:], in0=centred[:, :, A], in1=centred[:, :, A], op=ALU.mult)
+
+        for c in range(CHUNKS):
+            nc.tensor.matmul(
+                out=gram_ps[:, 0 : A + 1],
+                lhsT=centred[:, c, 0:A],
+                rhs=centred[:, c, :],
+                start=(c == 0),
+                stop=(c == CHUNKS - 1),
+            )
+        neg_c0_ps = psum_a.tile([P, CHUNKS], F32, tag="a")
         nc.tensor.matmul(out=neg_c0_ps[:], lhsT=neg_mean_f32[:], rhs=bc_sq[:], start=True, stop=True)
-        nc.vector.tensor_copy(
-            out=b_bc[:].rearrange("p (g t m) -> p g t m", g=PASSES, t=PACK),
-            in_=b_row[:].rearrange("p (g m t) -> p g t m", g=PASSES, t=PACK),
-        )
+        bc_rows = const.tile([P, F], F32)
+        for half in range(2):
+            bc_ps = psum_t.tile([P, BANK], F32, tag="t")
+            for c in range(CHUNKS // 2):
+                nc.tensor.transpose(
+                    bc_ps[:, c * P : (c + 1) * P],
+                    centred[:, half * CHUNKS // 2 + c, A : A + 1].to_broadcast([P, P]),
+                    ident_f32[:],
+                )
+            nc.scalar.copy(out=bc_rows[:, half * BANK : (half + 1) * BANK], in_=bc_ps[:])
         stat_hi = const.tile([P, STAT_COLS], BF16)
         nc.vector.tensor_copy(out=stat_hi[:], in_=gram_ps[:])
         stat_lo = const.tile([P, STAT_COLS], BF16)
@@ -167,23 +170,26 @@ def tile_actionbindingattention_pa_t_kernel(tc, actions, W_ae, b_ae, ln_g, ln_b,
         nc.vector.tensor_scalar(
             out=var_bias[:], in0=neg_var_b[:], scalar1=-1.0, scalar2=LN_EPS, op0=ALU.mult, op1=ALU.add
         )
+        gain = const.tile([P, CHUNKS], F32)
+        nc.vector.tensor_copy(out=gain[:], in_=g_bf[:].rearrange("p g t -> p (g t)"))
+        shift_f = const.tile([P, CHUNKS], F32)
+        nc.vector.tensor_copy(out=shift_f[:], in_=s_bf[:].rearrange("p g t -> p (g t)"))
 
         wv_grouped = const.tile([P, PASSES, F, PACK], BF16, align_bytes=64)
         wv_codes = const.tile([P, PASSES, F], U32, align_bytes=64)
         wv_scales = const.tile([P, PASSES, F], U8, align_bytes=64)
 
         def prepare_wv(oc):
-            wvT_ps = psum_o.tile([P, CHUNKS, P], BF16, tag="o")
-            for kc in range(CHUNKS):
-                g, t = divmod(kc, PACK)
-                k_first = g * PACK * P + t
-                nc.tensor.transpose(
-                    wvT_ps[:, kc, :], wv_nat[:, oc, k_first : (g + 1) * PACK * P : PACK], ident_bf[:]
-                )
+            words = wv_nat[:, oc, :].bitcast(F32)
+            wvT_ps = psum_o.tile([P, PASSES, PACK // 2, P], F32, tag="o")
+            for g in range(PASSES):
+                for u in range(PACK // 2):
+                    nc.tensor.transpose(wvT_ps[:, g, u, :], words[:, 2 * P * g + u : 2 * P * (g + 1) : 2], ident_f32[:])
             for g in range(PASSES):
                 nc.scalar.copy(
-                    out=wv_grouped[:, g, oc * P : (oc + 1) * P, :],
-                    in_=wvT_ps[:, g * PACK : (g + 1) * PACK, :].rearrange("p j o -> p o j"),
+                    out=wv_grouped[:, g, oc * P : (oc + 1) * P, :].rearrange("p o j -> p (o j)").bitcast(F32)
+                    .rearrange("p (o u) -> p o u", u=PACK // 2),
+                    in_=wvT_ps[:, g, :, :].rearrange("p u o -> p o u"),
                 )
             if (oc + 1) * P % BANK == 0:
                 cols = slice((oc + 1) * P - BANK, (oc + 1) * P)
@@ -194,8 +200,6 @@ def tile_actionbindingattention_pa_t_kernel(tc, actions, W_ae, b_ae, ln_g, ln_b,
                         in_=wv_grouped[:, g, cols, :].rearrange("p o j -> p (o j)"),
                     )
 
-        stat_ps = {}
-        f_var = {}
         rstd = {}
         bias_rows = {}
         n_tiles = {}
@@ -203,45 +207,33 @@ def tile_actionbindingattention_pa_t_kernel(tc, actions, W_ae, b_ae, ln_g, ln_b,
         grouped = {}
         quantised = {}
 
-        def statistics(pair):
-            group = pair * 2 // GROUP
-            if pair * 2 % GROUP == 0:
-                f_var_tile = stat_pool.tile([P, GROUP], F32)
-                f_var[group] = f_var_tile
-            y_ps = psum_y.tile([P, 2, STAT_COLS], F32, tag="y")
-            stat_ps[pair] = y_ps
-            for e in range(2):
-                nc.tensor.matmul(out=y_ps[:, e, :], lhsT=xT[:, 2 * pair + e, :], rhs=stat_hi[:], start=True, stop=False)
-                nc.tensor.matmul(out=y_ps[:, e, :], lhsT=xT[:, 2 * pair + e, :], rhs=stat_lo[:], start=False, stop=True)
-            for e in range(2):
-                tile_i = 2 * pair + e
+        def statistics(group):
+            f_var = stat_pool.tile([P, GROUP], F32)
+            neg_mean = stat_pool.tile([P, GROUP], F32)
+            y_ps = psum_y.tile([P, GROUP, STAT_COLS], F32, tag="y")
+            for r in range(GROUP):
+                tile_i = group * GROUP + r
+                nc.tensor.matmul(out=y_ps[:, r, :], lhsT=xT[:, tile_i, :], rhs=stat_hi[:], start=True, stop=False)
+                nc.tensor.matmul(out=y_ps[:, r, :], lhsT=xT[:, tile_i, :], rhs=stat_lo[:], start=False, stop=True)
+            nc.scalar.copy(out=neg_mean[:], in_=y_ps[:, :, A + 1])
+            for r in range(GROUP):
                 products = work.tile([P, A + 1], F32)
                 nc.vector.scalar_tensor_tensor(
                     out=products[:],
-                    in0=y_ps[:, e, 0 : A + 1],
+                    in0=y_ps[:, r, 0 : A + 1],
                     scalar=1.0,
-                    in1=x_aug[:, tile_i, 0 : A + 1],
+                    in1=x_aug[:, group * GROUP + r, 0 : A + 1],
                     op0=ALU.mult,
                     op1=ALU.mult,
-                    accum_out=f_var[group][:, tile_i % GROUP : tile_i % GROUP + 1],
+                    accum_out=f_var[:, r : r + 1],
                 )
-
-        def finish_statistics(group):
-            std = stat_pool.tile([P, GROUP], F32)
-            nc.scalar.activation(out=std[:], in_=f_var[group][:], func=ACT.Sqrt, bias=var_bias[:], scale=1.0 / F)
+            var = stat_pool.tile([P, GROUP], F32)
+            nc.gpsimd.tensor_scalar(
+                out=var[:], in0=f_var[:], scalar1=1.0 / F, scalar2=var_bias[:], op0=ALU.mult, op1=ALU.add
+            )
             rstd_tile = stat_pool.tile([P, GROUP], F32)
             rstd[group] = rstd_tile
-            nc.vector.reciprocal(out=rstd_tile[:], in_=std[:])
-            shift_t = stat_pool.tile([P, GROUP], F32)
-            for e in range(GROUP // 2):
-                nc.vector.scalar_tensor_tensor(
-                    out=shift_t[:, 2 * e : 2 * e + 2],
-                    in0=stat_ps[group * GROUP // 2 + e][:, :, A + 1],
-                    scalar=neg_bbar[:],
-                    in1=rstd_tile[:, 2 * e : 2 * e + 2],
-                    op0=ALU.add,
-                    op1=ALU.mult,
-                )
+            nc.gpsimd.tensor_tensor(out=rstd_tile[:], in0=var[:], in1=neg_half[:], op=ALU.pow)
             for r in range(GROUP):
                 bias_tile = bias_pool.tile([P, F], F32)
                 bias_rows[group * GROUP + r] = bias_tile
@@ -249,11 +241,11 @@ def tile_actionbindingattention_pa_t_kernel(tc, actions, W_ae, b_ae, ln_g, ln_b,
                     cols = slice(h * BANK, (h + 1) * BANK)
                     nc.gpsimd.tensor_scalar(
                         out=bias_tile[:, cols],
-                        in0=b_bc[:, cols],
-                        scalar1=rstd_tile[:, r : r + 1],
-                        scalar2=shift_t[:, r : r + 1],
-                        op0=ALU.mult,
-                        op1=ALU.add,
+                        in0=bc_rows[:, cols],
+                        scalar1=neg_mean[:, r : r + 1],
+                        scalar2=rstd_tile[:, r : r + 1],
+                        op0=ALU.add,
+                        op1=ALU.mult,
                     )
 
         def encode(tile_i):
@@ -272,30 +264,35 @@ def tile_actionbindingattention_pa_t_kernel(tc, actions, W_ae, b_ae, ln_g, ln_b,
                     op1=ALU.add,
                 )
 
-        def transpose_chunks(group, first, count):
-            if first == 0:
-                planes_tile = work.tile([P, CHUNKS, GROUP_TOKENS], BF16)
-                planes[group] = planes_tile
-            for c in range(first, first + count):
-                t_ps = psum_t.tile([P, GROUP_TOKENS], F32, tag="t")
-                for r in range(GROUP):
-                    nc.tensor.transpose(
-                        t_ps[:, r * P : (r + 1) * P], n_tiles[group * GROUP + r][:, c * P : (c + 1) * P], ident_f32[:]
+        def transpose_pass(group, g):
+            planes_tile = work.tile([P, PACK, GROUP_TOKENS], BF16)
+            planes[(group, g)] = planes_tile
+            for t0 in range(0, PACK, 2):
+                t_ps = psum_t.tile([P, 2, GROUP_TOKENS], F32, tag="t")
+                for e in range(2):
+                    c = g * PACK + t0 + e
+                    for r in range(GROUP):
+                        nc.tensor.transpose(
+                            t_ps[:, e, r * P : (r + 1) * P],
+                            n_tiles[group * GROUP + r][:, c * P : (c + 1) * P],
+                            ident_f32[:],
+                        )
+                for e in range(2):
+                    c = g * PACK + t0 + e
+                    nc.scalar.activation(
+                        out=planes_tile[:, t0 + e, :],
+                        in_=t_ps[:, e, :],
+                        func=ACT.Identity,
+                        scale=gain[:, c : c + 1],
+                        bias=shift_f[:, c : c + 1],
                     )
-                nc.scalar.activation(
-                    out=planes[group][:, c, :],
-                    in_=t_ps[:],
-                    func=ACT.Identity,
-                    scale=gain[:, c : c + 1],
-                    bias=shift_f[:, c : c + 1],
-                )
 
         def regroup(group, g):
-            grouped_tile = work.tile([P, GROUP_TOKENS, PACK], BF16, align_bytes=64, bufs=3)
+            grouped_tile = work.tile([P, GROUP_TOKENS, PACK], BF16, align_bytes=64)
             grouped[(group, g)] = grouped_tile
             nc.vector.tensor_copy(
                 out=grouped_tile[:].rearrange("p (c i) j -> p c j i", i=4),
-                in_=planes[group][:, g * PACK : (g + 1) * PACK, :].rearrange("p j (c i) -> p c j i", i=4),
+                in_=planes[(group, g)][:].rearrange("p j (c i) -> p c j i", i=4),
             )
 
         def quantise(group, g):
@@ -333,24 +330,35 @@ def tile_actionbindingattention_pa_t_kernel(tc, actions, W_ae, b_ae, ln_g, ln_b,
                     nc.scalar.copy(out=o_sb[:, cols], in_=o_ps[:])
             nc.sync.dma_start(out=out_dram[:, tile_i, :], in_=o_sb[:])
 
-        chunks_a_slot = CHUNKS // GROUP
+        wT = const.tile([P, F], BF16)
+
+        def transpose_weight():
+            wT_ps = psum_o.tile([P, CHUNKS, P], BF16, tag="o")
+            for c in range(CHUNKS):
+                nc.tensor.transpose(wT_ps[:, c, :], w_nat[:, c, :], ident_bf[:])
+            nc.scalar.copy(out=wT[:], in_=wT_ps[:].rearrange("p c f -> p (c f)"))
+
         for slot in range(-STATS_LEAD, TILES + PROJECT_LAG):
             if 0 <= slot - PROJECT_LAG:
                 project(slot - PROJECT_LAG)
             if 0 <= slot < TILES:
                 encode(slot)
             ahead = slot + STATS_LEAD
-            if ahead < TILES and ahead % 2 == 0:
-                statistics(ahead // 2)
-            if ahead < TILES and ahead % GROUP == GROUP - 1:
-                finish_statistics(ahead // GROUP)
-            if 0 <= slot < CHUNKS:
-                prepare_wv(slot)
+            if ahead < TILES and ahead % GROUP == 0:
+                statistics(ahead // GROUP)
+            if 0 <= slot < CHUNKS // 2:
+                prepare_wv(2 * slot)
+                prepare_wv(2 * slot + 1)
+            if slot == -STATS_LEAD:
+                transpose_weight()
+            if slot in (-3, 2, 10):
+                transpose_actions({-3: 1, 2: 2, 10: 3}[slot])
             behind = slot - TRANSPOSE_LAG
             if 0 <= behind < TILES:
-                transpose_chunks(behind // GROUP, behind % GROUP * chunks_a_slot, chunks_a_slot)
+                transpose_pass(behind // GROUP, behind % GROUP)
             behind = slot - REGROUP_LAG
-            if 0 <= behind < TILES and behind % 2 == 0:
-                regroup(behind // GROUP, behind % GROUP // 2)
-            if 0 <= behind < TILES and behind % 2 == 1:
-                quantise(behind // GROUP, behind % GROUP // 2)
+            if 0 <= behind < TILES:
+                regroup(behind // GROUP, behind % GROUP)
+            behind = slot - QUANTISE_LAG
+            if 0 <= behind < TILES:
+                quantise(behind // GROUP, behind % GROUP)

@@ -30,6 +30,8 @@ X_PITCH = A + 32
 STAT_COLS = A + 2
 
 STATS_LEAD = 6
+DEVIATION_LEAD = 4
+BIAS_LEAD = 2
 TRANSPOSE_LAG = GROUP
 REGROUP_LAG = TRANSPOSE_LAG + 1
 QUANTISE_LAG = REGROUP_LAG + 1
@@ -46,8 +48,8 @@ def tile_actionbindingattention_pa_t_kernel(tc, actions, W_ae, b_ae, ln_g, ln_b,
     with ExitStack() as ctx:
         ctx.enter_context(tc.manual_schedule())
         const = ctx.enter_context(tc.tile_pool(name="const", bufs=1))
-        stat_pool = ctx.enter_context(tc.tile_pool(name="stat_pool", bufs=STATS_LEAD // GROUP + 2))
-        bias_pool = ctx.enter_context(tc.tile_pool(name="bias_pool", bufs=STATS_LEAD + 2))
+        stat_pool = ctx.enter_context(tc.tile_pool(name="stat_pool", bufs=STATS_LEAD))
+        bias_pool = ctx.enter_context(tc.tile_pool(name="bias_pool", bufs=BIAS_LEAD + 2))
         n_pool = ctx.enter_context(tc.tile_pool(name="n_pool", bufs=8))
         work = ctx.enter_context(tc.tile_pool(name="work", bufs=3))
         o_pool = ctx.enter_context(tc.tile_pool(name="o_pool", bufs=4))
@@ -87,12 +89,12 @@ def tile_actionbindingattention_pa_t_kernel(tc, actions, W_ae, b_ae, ln_g, ln_b,
         nc.vector.memset(neg_mean_bf[:], -1.0 / F)
         neg_mean_f32 = const.tile([P, P], F32)
         nc.vector.memset(neg_mean_f32[:], -1.0 / F)
+        warm = const.tile([P, 1], F32)
+        nc.scalar.activation(out=warm[:], in_=neg_mean_f32[:, 0:1], func=ACT.Sqrt, scale=-1.0)
         ident_bf = const.tile([P, P], BF16)
         make_identity(nc, ident_bf[:])
         ident_f32 = const.tile([P, P], F32)
         make_identity(nc, ident_f32[:])
-        neg_half = const.tile([P, GROUP], F32)
-        nc.gpsimd.memset(neg_half[:], -0.5)
         nc.vector.memset(x_aug[:, :, A : A + 1], 2.0)
 
         neg_wbar_ps = psum_y.tile([P, A], F32, tag="y")
@@ -200,7 +202,10 @@ def tile_actionbindingattention_pa_t_kernel(tc, actions, W_ae, b_ae, ln_g, ln_b,
                         in_=wv_grouped[:, g, cols, :].rearrange("p o j -> p (o j)"),
                     )
 
+        f_vars = {}
+        stds = {}
         rstd = {}
+        neg_means = {}
         bias_rows = {}
         n_tiles = {}
         planes = {}
@@ -227,26 +232,29 @@ def tile_actionbindingattention_pa_t_kernel(tc, actions, W_ae, b_ae, ln_g, ln_b,
                     op1=ALU.mult,
                     accum_out=f_var[:, r : r + 1],
                 )
-            var = stat_pool.tile([P, GROUP], F32)
+            f_vars[group] = f_var
+            neg_means[group] = neg_mean
+
+        def standard_deviation(group):
+            std = stat_pool.tile([P, GROUP], F32)
+            nc.scalar.activation(out=std[:], in_=f_vars[group][:], func=ACT.Sqrt, bias=var_bias[:], scale=1.0 / F)
+            stds[group] = std
+
+        def make_bias_row(tile_i):
+            group, r = divmod(tile_i, GROUP)
+            rstd_tile = stat_pool.tile([P, 1], F32)
+            rstd[tile_i] = rstd_tile
+            nc.vector.reciprocal(out=rstd_tile[:], in_=stds[group][:, r : r + 1])
+            bias_tile = bias_pool.tile([P, F], F32)
+            bias_rows[tile_i] = bias_tile
             nc.gpsimd.tensor_scalar(
-                out=var[:], in0=f_var[:], scalar1=1.0 / F, scalar2=var_bias[:], op0=ALU.mult, op1=ALU.add
+                out=bias_tile[:],
+                in0=bc_rows[:],
+                scalar1=neg_means[group][:, r : r + 1],
+                scalar2=rstd_tile[:],
+                op0=ALU.add,
+                op1=ALU.mult,
             )
-            rstd_tile = stat_pool.tile([P, GROUP], F32)
-            rstd[group] = rstd_tile
-            nc.gpsimd.tensor_tensor(out=rstd_tile[:], in0=var[:], in1=neg_half[:], op=ALU.pow)
-            for r in range(GROUP):
-                bias_tile = bias_pool.tile([P, F], F32)
-                bias_rows[group * GROUP + r] = bias_tile
-                for h in range(HALVES):
-                    cols = slice(h * BANK, (h + 1) * BANK)
-                    nc.gpsimd.tensor_scalar(
-                        out=bias_tile[:, cols],
-                        in0=bc_rows[:, cols],
-                        scalar1=neg_mean[:, r : r + 1],
-                        scalar2=rstd_tile[:, r : r + 1],
-                        op0=ALU.add,
-                        op1=ALU.mult,
-                    )
 
         def encode(tile_i):
             n_sb = n_pool.tile([P, F], F32)
@@ -258,7 +266,7 @@ def tile_actionbindingattention_pa_t_kernel(tc, actions, W_ae, b_ae, ln_g, ln_b,
                 nc.vector.scalar_tensor_tensor(
                     out=n_sb[:, cols],
                     in0=a_ps[:],
-                    scalar=rstd[tile_i // GROUP][:, tile_i % GROUP : tile_i % GROUP + 1],
+                    scalar=rstd[tile_i][:],
                     in1=bias_rows[tile_i][:, cols],
                     op0=ALU.mult,
                     op1=ALU.add,
@@ -346,13 +354,16 @@ def tile_actionbindingattention_pa_t_kernel(tc, actions, W_ae, b_ae, ln_g, ln_b,
             ahead = slot + STATS_LEAD
             if ahead < TILES and ahead % GROUP == 0:
                 statistics(ahead // GROUP)
+            ahead = slot + DEVIATION_LEAD
+            if 0 <= ahead < TILES and ahead % GROUP == 0:
+                standard_deviation(ahead // GROUP)
             if 0 <= slot < CHUNKS // 2:
                 prepare_wv(2 * slot)
                 prepare_wv(2 * slot + 1)
             if slot == -STATS_LEAD:
                 transpose_weight()
-            if slot in (-3, 2, 10):
-                transpose_actions({-3: 1, 2: 2, 10: 3}[slot])
+            if slot in (-3, 4, 12):
+                transpose_actions({-3: 1, 4: 2, 12: 3}[slot])
             behind = slot - TRANSPOSE_LAG
             if 0 <= behind < TILES:
                 transpose_pass(behind // GROUP, behind % GROUP)
@@ -362,3 +373,5 @@ def tile_actionbindingattention_pa_t_kernel(tc, actions, W_ae, b_ae, ln_g, ln_b,
             behind = slot - QUANTISE_LAG
             if 0 <= behind < TILES:
                 quantise(behind // GROUP, behind % GROUP)
+            if 0 <= slot + BIAS_LEAD < TILES:
+                make_bias_row(slot + BIAS_LEAD)

@@ -30,6 +30,7 @@ X_PITCH = A + 32
 STAT_COLS = A + 2
 
 STATS_LEAD = 6
+WARM_UP = 5
 DEVIATION_LEAD = 4
 BIAS_LEAD = 2
 TRANSPOSE_LAG = GROUP
@@ -68,24 +69,23 @@ def tile_actionbindingattention_pa_t_kernel(tc, actions, W_ae, b_ae, ln_g, ln_b,
         b_bf = const.tile([P, PASSES, PACK], BF16)
         nc.sync.dma_start(out=b_bf[:], in_=b_ae.rearrange("(g p t) -> p g t", g=PASSES, t=PACK))
         x_aug = const.tile([P, TILES, X_PITCH], BF16)
-        x_piece = TILES // 4
 
-        def load_actions(q):
-            tiles_q = slice(q * x_piece, (q + 1) * x_piece)
-            nc.sync.dma_start(out=x_aug[:, tiles_q, 0:A], in_=x_dram[:, tiles_q, :])
+        def load_actions(first, end):
+            nc.sync.dma_start(out=x_aug[:, first:end, 0:A], in_=x_dram[:, first:end, :])
 
-        load_actions(0)
+        load_actions(0, GROUP)
         for cols_bf, vec in ((g_bf, ln_g), (s_bf, ln_b)):
             nc.sync.dma_start(out=cols_bf[:], in_=vec.rearrange("(g p t) -> p g t", g=PASSES, t=PACK))
-        load_actions(1)
+        load_actions(GROUP, 8)
+        load_actions(8, 16)
         wv_nat = const.tile([P, CHUNKS, F], BF16)
         wv_dram = Wv.rearrange("(oc p) k -> p oc k", p=P)
         for q in range(4):
             nc.sync.dma_start(out=wv_nat[:, 2 * q : 2 * q + 2, :], in_=wv_dram[:, 2 * q : 2 * q + 2, :])
             if q in (1, 2):
-                load_actions(q + 1)
+                load_actions(8 * q + 8, 8 * q + 16)
 
-        neg_mean_bf = const.tile([P, P], BF16)
+        neg_mean_bf = const.tile([P, BANK], BF16)
         nc.vector.memset(neg_mean_bf[:], -1.0 / F)
         neg_mean_f32 = const.tile([P, P], F32)
         nc.vector.memset(neg_mean_f32[:], -1.0 / F)
@@ -96,16 +96,34 @@ def tile_actionbindingattention_pa_t_kernel(tc, actions, W_ae, b_ae, ln_g, ln_b,
         ident_f32 = const.tile([P, P], F32)
         make_identity(nc, ident_f32[:])
         nc.vector.memset(x_aug[:, :, A : A + 1], 2.0)
+        for i in range(WARM_UP):
+            warm_ps = psum_t.tile([P, BANK], F32, tag="t")
+            nc.tensor.matmul(out=warm_ps[:], lhsT=neg_mean_bf[:, 0:P], rhs=neg_mean_bf[:], start=True, stop=True)
 
-        neg_wbar_ps = psum_y.tile([P, A], F32, tag="y")
-        for c in range(CHUNKS):
-            nc.tensor.matmul(
-                out=neg_wbar_ps[:], lhsT=neg_mean_bf[:], rhs=w_nat[:, c, :], start=(c == 0), stop=(c == CHUNKS - 1)
-            )
         b_cols = const.tile([P, CHUNKS], F32)
         nc.vector.tensor_copy(out=b_cols[:], in_=b_bf[:].rearrange("p g t -> p (g t)"))
+        neg_wbar_ps = psum_y.tile([P, A], F32, tag="y")
         neg_b_ps = psum_y.tile([P, CHUNKS], F32, tag="y")
-        nc.tensor.matmul(out=neg_b_ps[:], lhsT=neg_mean_f32[:], rhs=b_cols[:], start=True, stop=True)
+        for c in range(CHUNKS):
+            nc.tensor.matmul(
+                out=neg_wbar_ps[:], lhsT=neg_mean_bf[:, 0:P], rhs=w_nat[:, c, :], start=(c == 0), stop=(c == CHUNKS - 1)
+            )
+            if c == CHUNKS // 2:
+                nc.tensor.matmul(out=neg_b_ps[:], lhsT=neg_mean_f32[:], rhs=b_cols[:], start=True, stop=True)
+        neg_bbar = const.tile([P, 1], F32)
+        nc.vector.tensor_reduce(out=neg_bbar[:], in_=neg_b_ps[:], axis=AXIS.X, op=ALU.add)
+        centred = const.tile([P, CHUNKS, A + 1], F32)
+        nc.vector.tensor_scalar(out=centred[:, :, A], in0=b_cols[:], scalar1=neg_bbar[:], scalar2=None, op0=ALU.add)
+        for half in range(2):
+            chunks = slice(half * CHUNKS // 2, (half + 1) * CHUNKS // 2)
+            nc.vector.tensor_tensor(
+                out=centred[:, chunks, 0:A],
+                in0=w_nat[:, chunks, :],
+                in1=neg_wbar_ps[:].unsqueeze(1).to_broadcast([P, CHUNKS // 2, A]),
+                op=ALU.add,
+            )
+        bc_sq = const.tile([P, CHUNKS], F32)
+        nc.vector.tensor_tensor(out=bc_sq[:], in0=centred[:, :, A], in1=centred[:, :, A], op=ALU.mult)
         gram_ps = psum_a.tile([P, STAT_COLS], F32, tag="a")
         for c in range(CHUNKS):
             nc.tensor.matmul(
@@ -117,31 +135,13 @@ def tile_actionbindingattention_pa_t_kernel(tc, actions, W_ae, b_ae, ln_g, ln_b,
             )
         xT = const.tile([P, TILES, P], BF16)
 
-        def transpose_actions(q):
+        def transpose_actions(first, end):
             xT_ps = psum_o.tile([P, CHUNKS, P], BF16, tag="o")
-            for r in range(CHUNKS):
-                nc.tensor.transpose(xT_ps[:, r, :], x_aug[:, q * CHUNKS + r, 0:A], ident_bf[:])
-            nc.scalar.copy(out=xT[:, q * CHUNKS : (q + 1) * CHUNKS, :], in_=xT_ps[:])
+            for i in range(first, end):
+                nc.tensor.transpose(xT_ps[:, i - first, :], x_aug[:, i, 0:A], ident_bf[:])
+            nc.scalar.copy(out=xT[:, first:end, :], in_=xT_ps[:, 0 : end - first, :])
 
-        transpose_actions(0)
-        centred = const.tile([P, CHUNKS, A + 1], F32)
-        for half in range(2):
-            chunks = slice(half * CHUNKS // 2, (half + 1) * CHUNKS // 2)
-            nc.vector.tensor_tensor(
-                out=centred[:, chunks, 0:A],
-                in0=w_nat[:, chunks, :],
-                in1=neg_wbar_ps[:].unsqueeze(1).to_broadcast([P, CHUNKS // 2, A]),
-                op=ALU.add,
-            )
-            if half == 0:
-                neg_bbar = const.tile([P, 1], F32)
-                nc.vector.tensor_reduce(out=neg_bbar[:], in_=neg_b_ps[:], axis=AXIS.X, op=ALU.add)
-                nc.vector.tensor_scalar(
-                    out=centred[:, :, A], in0=b_cols[:], scalar1=neg_bbar[:], scalar2=None, op0=ALU.add
-                )
-        bc_sq = const.tile([P, CHUNKS], F32)
-        nc.vector.tensor_tensor(out=bc_sq[:], in0=centred[:, :, A], in1=centred[:, :, A], op=ALU.mult)
-
+        transpose_actions(0, GROUP)
         for c in range(CHUNKS):
             nc.tensor.matmul(
                 out=gram_ps[:, 0 : A + 1],
@@ -247,7 +247,8 @@ def tile_actionbindingattention_pa_t_kernel(tc, actions, W_ae, b_ae, ln_g, ln_b,
             nc.vector.reciprocal(out=rstd_tile[:], in_=stds[group][:, r : r + 1])
             bias_tile = bias_pool.tile([P, F], F32)
             bias_rows[tile_i] = bias_tile
-            nc.gpsimd.tensor_scalar(
+            engine = nc.vector if group == 0 else nc.gpsimd
+            engine.tensor_scalar(
                 out=bias_tile[:],
                 in0=bc_rows[:],
                 scalar1=neg_means[group][:, r : r + 1],
@@ -346,24 +347,33 @@ def tile_actionbindingattention_pa_t_kernel(tc, actions, W_ae, b_ae, ln_g, ln_b,
                 nc.tensor.transpose(wT_ps[:, c, :], w_nat[:, c, :], ident_bf[:])
             nc.scalar.copy(out=wT[:], in_=wT_ps[:].rearrange("p c f -> p (c f)"))
 
-        for slot in range(-STATS_LEAD, TILES + PROJECT_LAG):
+        statistics(0)
+        standard_deviation(0)
+        make_bias_row(0)
+        make_bias_row(1)
+        transpose_weight()
+        transpose_actions(GROUP, 8)
+        for group in range(1, STATS_LEAD // GROUP):
+            statistics(group)
+            if (group + 1) * GROUP <= DEVIATION_LEAD:
+                standard_deviation(group)
+        transpose_actions(8, 16)
+        for slot in range(TILES + PROJECT_LAG):
             if 0 <= slot - PROJECT_LAG:
                 project(slot - PROJECT_LAG)
-            if 0 <= slot < TILES:
+            if slot < TILES:
                 encode(slot)
             ahead = slot + STATS_LEAD
             if ahead < TILES and ahead % GROUP == 0:
                 statistics(ahead // GROUP)
             ahead = slot + DEVIATION_LEAD
-            if 0 <= ahead < TILES and ahead % GROUP == 0:
+            if ahead < TILES and ahead % GROUP == 0:
                 standard_deviation(ahead // GROUP)
-            if 0 <= slot < CHUNKS // 2:
+            if slot < CHUNKS // 2:
                 prepare_wv(2 * slot)
                 prepare_wv(2 * slot + 1)
-            if slot == -STATS_LEAD:
-                transpose_weight()
-            if slot in (-3, 4, 12):
-                transpose_actions({-3: 1, 4: 2, 12: 3}[slot])
+            if slot in (4, 12):
+                transpose_actions(slot + 12, slot + 20)
             behind = slot - TRANSPOSE_LAG
             if 0 <= behind < TILES:
                 transpose_pass(behind // GROUP, behind % GROUP)
@@ -373,5 +383,5 @@ def tile_actionbindingattention_pa_t_kernel(tc, actions, W_ae, b_ae, ln_g, ln_b,
             behind = slot - QUANTISE_LAG
             if 0 <= behind < TILES:
                 quantise(behind // GROUP, behind % GROUP)
-            if 0 <= slot + BIAS_LEAD < TILES:
+            if slot + BIAS_LEAD < TILES:
                 make_bias_row(slot + BIAS_LEAD)

@@ -29,9 +29,9 @@ HALVES = F // BANK
 X_PITCH = A + 32
 STAT_COLS = A + 2
 
-STATS_LEAD = 6
-WARM_UP = 5
-DEVIATION_LEAD = 4
+STATS_LEAD = 4
+WARM_UP = 12
+DEVIATION_LEAD = 3
 BIAS_LEAD = 2
 TRANSPOSE_LAG = GROUP
 REGROUP_LAG = TRANSPOSE_LAG + 1
@@ -77,18 +77,21 @@ def tile_actionbindingattention_pa_t_kernel(tc, actions, W_ae, b_ae, ln_g, ln_b,
         for cols_bf, vec in ((g_bf, ln_g), (s_bf, ln_b)):
             nc.sync.dma_start(out=cols_bf[:], in_=vec.rearrange("(g p t) -> p g t", g=PASSES, t=PACK))
         load_actions(GROUP, 8)
-        load_actions(8, 16)
         wv_nat = const.tile([P, CHUNKS, F], BF16)
         wv_dram = Wv.rearrange("(oc p) k -> p oc k", p=P)
         for q in range(4):
             nc.sync.dma_start(out=wv_nat[:, 2 * q : 2 * q + 2, :], in_=wv_dram[:, 2 * q : 2 * q + 2, :])
-            if q in (1, 2):
-                load_actions(8 * q + 8, 8 * q + 16)
+            if q in (0, 1, 3):
+                load_actions({0: 8, 1: 16, 3: 24}[q], {0: 16, 1: 24, 3: 32}[q])
 
-        neg_mean_bf = const.tile([P, BANK], BF16)
+        neg_mean_bf = const.tile([P, P], BF16)
         nc.vector.memset(neg_mean_bf[:], -1.0 / F)
         neg_mean_f32 = const.tile([P, P], F32)
         nc.vector.memset(neg_mean_f32[:], -1.0 / F)
+        side = const.tile([P, CHUNKS, 2], BF16)
+        nc.vector.memset(side[:], -1.0 / F)
+        neg_b8 = const.tile([P, 2], F32)
+        nc.vector.memset(neg_b8[:], 0.0)
         warm = const.tile([P, 1], F32)
         nc.scalar.activation(out=warm[:], in_=neg_mean_f32[:, 0:1], func=ACT.Sqrt, scale=-1.0)
         ident_bf = const.tile([P, P], BF16)
@@ -96,43 +99,31 @@ def tile_actionbindingattention_pa_t_kernel(tc, actions, W_ae, b_ae, ln_g, ln_b,
         ident_f32 = const.tile([P, P], F32)
         make_identity(nc, ident_f32[:])
         nc.vector.memset(x_aug[:, :, A : A + 1], 2.0)
+        warm_ps = psum_t.tile([P, P], F32, tag="t")
         for i in range(WARM_UP):
-            warm_ps = psum_t.tile([P, BANK], F32, tag="t")
-            nc.tensor.matmul(out=warm_ps[:], lhsT=neg_mean_bf[:, 0:P], rhs=neg_mean_bf[:], start=True, stop=True)
+            nc.tensor.matmul(out=warm_ps[:], lhsT=neg_mean_bf[:], rhs=neg_mean_bf[:], start=True, stop=True)
 
         b_cols = const.tile([P, CHUNKS], F32)
         nc.vector.tensor_copy(out=b_cols[:], in_=b_bf[:].rearrange("p g t -> p (g t)"))
+        nc.vector.tensor_copy(out=side[:, :, 0], in_=b_bf[:].rearrange("p g t -> p (g t)"))
         neg_wbar_ps = psum_y.tile([P, A], F32, tag="y")
-        neg_b_ps = psum_y.tile([P, CHUNKS], F32, tag="y")
         for c in range(CHUNKS):
             nc.tensor.matmul(
-                out=neg_wbar_ps[:], lhsT=neg_mean_bf[:, 0:P], rhs=w_nat[:, c, :], start=(c == 0), stop=(c == CHUNKS - 1)
+                out=neg_wbar_ps[:], lhsT=neg_mean_bf[:], rhs=w_nat[:, c, :], start=(c == 0), stop=(c == CHUNKS - 1)
             )
-            if c == CHUNKS // 2:
-                nc.tensor.matmul(out=neg_b_ps[:], lhsT=neg_mean_f32[:], rhs=b_cols[:], start=True, stop=True)
+        neg_b_ps = psum_y.tile([P, CHUNKS], F32, tag="y")
+        nc.tensor.matmul(out=neg_b_ps[:], lhsT=neg_mean_f32[:], rhs=b_cols[:], start=True, stop=True)
+        neg_w = const.tile([P, A], F32)
+        nc.vector.tensor_copy(out=neg_w[:], in_=neg_wbar_ps[:])
+        w8 = const.tile([P, A], F32)
+        nc.vector.tensor_scalar(out=w8[:], in0=neg_wbar_ps[:], scalar1=-F / P, scalar2=None, op0=ALU.mult)
         neg_bbar = const.tile([P, 1], F32)
         nc.vector.tensor_reduce(out=neg_bbar[:], in_=neg_b_ps[:], axis=AXIS.X, op=ALU.add)
-        centred = const.tile([P, CHUNKS, A + 1], F32)
-        nc.vector.tensor_scalar(out=centred[:, :, A], in0=b_cols[:], scalar1=neg_bbar[:], scalar2=None, op0=ALU.add)
-        for half in range(2):
-            chunks = slice(half * CHUNKS // 2, (half + 1) * CHUNKS // 2)
-            nc.vector.tensor_tensor(
-                out=centred[:, chunks, 0:A],
-                in0=w_nat[:, chunks, :],
-                in1=neg_wbar_ps[:].unsqueeze(1).to_broadcast([P, CHUNKS // 2, A]),
-                op=ALU.add,
-            )
+        nc.vector.tensor_scalar(out=neg_b8[:, 0:1], in0=neg_bbar[:], scalar1=-F / P, scalar2=None, op0=ALU.mult)
+        bc_cols = const.tile([P, CHUNKS], F32)
+        nc.vector.tensor_scalar(out=bc_cols[:], in0=b_cols[:], scalar1=neg_bbar[:], scalar2=None, op0=ALU.add)
         bc_sq = const.tile([P, CHUNKS], F32)
-        nc.vector.tensor_tensor(out=bc_sq[:], in0=centred[:, :, A], in1=centred[:, :, A], op=ALU.mult)
-        gram_ps = psum_a.tile([P, STAT_COLS], F32, tag="a")
-        for c in range(CHUNKS):
-            nc.tensor.matmul(
-                out=gram_ps[:, A + 1 : A + 2],
-                lhsT=w_nat[:, c, :],
-                rhs=neg_mean_bf[:, 0:1],
-                start=(c == 0),
-                stop=(c == CHUNKS - 1),
-            )
+        nc.vector.tensor_tensor(out=bc_sq[:], in0=bc_cols[:], in1=bc_cols[:], op=ALU.mult)
         xT = const.tile([P, TILES, P], BF16)
 
         def transpose_actions(first, end):
@@ -141,27 +132,20 @@ def tile_actionbindingattention_pa_t_kernel(tc, actions, W_ae, b_ae, ln_g, ln_b,
                 nc.tensor.transpose(xT_ps[:, i - first, :], x_aug[:, i, 0:A], ident_bf[:])
             nc.scalar.copy(out=xT[:, first:end, :], in_=xT_ps[:, 0 : end - first, :])
 
+        gram_ps = psum_a.tile([P, STAT_COLS], F32, tag="a")
+        for cols, moving, neg_outer in ((slice(0, A), w_nat, w8), (slice(A, STAT_COLS), side, neg_b8)):
+            for c in range(CHUNKS):
+                nc.tensor.matmul(
+                    out=gram_ps[:, cols], lhsT=w_nat[:, c, :], rhs=moving[:, c, :], start=(c == 0), stop=False
+                )
+            nc.tensor.matmul(out=gram_ps[:, cols], lhsT=neg_w[:], rhs=neg_outer[:], start=False, stop=True)
         transpose_actions(0, GROUP)
+        wT = const.tile([P, F], BF16)
+        wT_ps = psum_o.tile([P, CHUNKS, P], BF16, tag="o")
         for c in range(CHUNKS):
-            nc.tensor.matmul(
-                out=gram_ps[:, 0 : A + 1],
-                lhsT=centred[:, c, 0:A],
-                rhs=centred[:, c, :],
-                start=(c == 0),
-                stop=(c == CHUNKS - 1),
-            )
+            nc.tensor.transpose(wT_ps[:, c, :], w_nat[:, c, :], ident_bf[:])
         neg_c0_ps = psum_a.tile([P, CHUNKS], F32, tag="a")
         nc.tensor.matmul(out=neg_c0_ps[:], lhsT=neg_mean_f32[:], rhs=bc_sq[:], start=True, stop=True)
-        bc_rows = const.tile([P, F], F32)
-        for half in range(2):
-            bc_ps = psum_t.tile([P, BANK], F32, tag="t")
-            for c in range(CHUNKS // 2):
-                nc.tensor.transpose(
-                    bc_ps[:, c * P : (c + 1) * P],
-                    centred[:, half * CHUNKS // 2 + c, A : A + 1].to_broadcast([P, P]),
-                    ident_f32[:],
-                )
-            nc.scalar.copy(out=bc_rows[:, half * BANK : (half + 1) * BANK], in_=bc_ps[:])
         stat_hi = const.tile([P, STAT_COLS], BF16)
         nc.vector.tensor_copy(out=stat_hi[:], in_=gram_ps[:])
         stat_lo = const.tile([P, STAT_COLS], BF16)
@@ -172,6 +156,20 @@ def tile_actionbindingattention_pa_t_kernel(tc, actions, W_ae, b_ae, ln_g, ln_b,
         nc.vector.tensor_scalar(
             out=var_bias[:], in0=neg_var_b[:], scalar1=-1.0, scalar2=LN_EPS, op0=ALU.mult, op1=ALU.add
         )
+        nc.vector.tensor_copy(out=wT[:], in_=wT_ps[:].rearrange("p c f -> p (c f)"))
+        bc_rows = const.tile([P, F], F32)
+
+        def spread_bias():
+            for half in range(2):
+                bc_ps = psum_t.tile([P, BANK], F32, tag="t")
+                for c in range(CHUNKS // 2):
+                    nc.tensor.transpose(
+                        bc_ps[:, c * P : (c + 1) * P],
+                        bc_cols[:, half * CHUNKS // 2 + c : half * CHUNKS // 2 + c + 1].to_broadcast([P, P]),
+                        ident_f32[:],
+                    )
+                nc.scalar.copy(out=bc_rows[:, half * BANK : (half + 1) * BANK], in_=bc_ps[:])
+
         gain = const.tile([P, CHUNKS], F32)
         nc.vector.tensor_copy(out=gain[:], in_=g_bf[:].rearrange("p g t -> p (g t)"))
         shift_f = const.tile([P, CHUNKS], F32)
@@ -257,21 +255,21 @@ def tile_actionbindingattention_pa_t_kernel(tc, actions, W_ae, b_ae, ln_g, ln_b,
                 op1=ALU.mult,
             )
 
-        def encode(tile_i):
-            n_sb = n_pool.tile([P, F], F32)
-            n_tiles[tile_i] = n_sb
-            for h in range(HALVES):
-                cols = slice(h * BANK, (h + 1) * BANK)
-                a_ps = psum_a.tile([P, BANK], F32, tag="a")
-                nc.tensor.matmul(out=a_ps[:], lhsT=xT[:, tile_i, :], rhs=wT[:, cols], start=True, stop=True)
-                nc.vector.scalar_tensor_tensor(
-                    out=n_sb[:, cols],
-                    in0=a_ps[:],
-                    scalar=rstd[tile_i][:],
-                    in1=bias_rows[tile_i][:, cols],
-                    op0=ALU.mult,
-                    op1=ALU.add,
-                )
+        def encode(tile_i, h):
+            if h == 0:
+                n_sb = n_pool.tile([P, F], F32)
+                n_tiles[tile_i] = n_sb
+            cols = slice(h * BANK, (h + 1) * BANK)
+            a_ps = psum_a.tile([P, BANK], F32, tag="a")
+            nc.tensor.matmul(out=a_ps[:], lhsT=xT[:, tile_i, :], rhs=wT[:, cols], start=True, stop=True)
+            nc.vector.scalar_tensor_tensor(
+                out=n_tiles[tile_i][:, cols],
+                in0=a_ps[:],
+                scalar=rstd[tile_i][:],
+                in1=bias_rows[tile_i][:, cols],
+                op0=ALU.mult,
+                op1=ALU.add,
+            )
 
         def transpose_pass(group, g):
             planes_tile = work.tile([P, PACK, GROUP_TOKENS], BF16)
@@ -339,30 +337,21 @@ def tile_actionbindingattention_pa_t_kernel(tc, actions, W_ae, b_ae, ln_g, ln_b,
                     nc.scalar.copy(out=o_sb[:, cols], in_=o_ps[:])
             nc.sync.dma_start(out=out_dram[:, tile_i, :], in_=o_sb[:])
 
-        wT = const.tile([P, F], BF16)
-
-        def transpose_weight():
-            wT_ps = psum_o.tile([P, CHUNKS, P], BF16, tag="o")
-            for c in range(CHUNKS):
-                nc.tensor.transpose(wT_ps[:, c, :], w_nat[:, c, :], ident_bf[:])
-            nc.scalar.copy(out=wT[:], in_=wT_ps[:].rearrange("p c f -> p (c f)"))
-
+        spread_bias()
         statistics(0)
         standard_deviation(0)
+        transpose_actions(GROUP, 8)
         make_bias_row(0)
         make_bias_row(1)
-        transpose_weight()
-        transpose_actions(GROUP, 8)
-        for group in range(1, STATS_LEAD // GROUP):
-            statistics(group)
-            if (group + 1) * GROUP <= DEVIATION_LEAD:
-                standard_deviation(group)
-        transpose_actions(8, 16)
+        statistics(1)
+        standard_deviation(1)
         for slot in range(TILES + PROJECT_LAG):
+            if 0 <= slot - 1 < TILES:
+                encode(slot - 1, 1)
             if 0 <= slot - PROJECT_LAG:
                 project(slot - PROJECT_LAG)
             if slot < TILES:
-                encode(slot)
+                encode(slot, 0)
             ahead = slot + STATS_LEAD
             if ahead < TILES and ahead % GROUP == 0:
                 statistics(ahead // GROUP)
@@ -372,8 +361,8 @@ def tile_actionbindingattention_pa_t_kernel(tc, actions, W_ae, b_ae, ln_g, ln_b,
             if slot < CHUNKS // 2:
                 prepare_wv(2 * slot)
                 prepare_wv(2 * slot + 1)
-            if slot in (4, 12):
-                transpose_actions(slot + 12, slot + 20)
+            if slot in (2, 10, 18):
+                transpose_actions(slot + 6, slot + 14)
             behind = slot - TRANSPOSE_LAG
             if 0 <= behind < TILES:
                 transpose_pass(behind // GROUP, behind % GROUP)

@@ -54,10 +54,10 @@ def tile_actionbindingattention_pa_t_kernel(tc, actions, W_ae, b_ae, ln_g, ln_b,
         n_pool = ctx.enter_context(tc.tile_pool(name="n_pool", bufs=8))
         work = ctx.enter_context(tc.tile_pool(name="work", bufs=3))
         o_pool = ctx.enter_context(tc.tile_pool(name="o_pool", bufs=4))
-        psum_y = ctx.enter_context(tc.psum_pool(name="psum_y", bufs=2))
+        psum_y = ctx.enter_context(tc.psum_pool(name="psum_y", bufs=1))
         psum_a = ctx.enter_context(tc.psum_pool(name="psum_a", bufs=2))
         psum_t = ctx.enter_context(tc.psum_pool(name="psum_t", bufs=2))
-        psum_o = ctx.enter_context(tc.psum_pool(name="psum_o", bufs=2))
+        psum_o = ctx.enter_context(tc.psum_pool(name="psum_o", bufs=3))
 
         w_nat = const.tile([P, CHUNKS, A], BF16)
         nc.sync.dma_start(
@@ -111,7 +111,7 @@ def tile_actionbindingattention_pa_t_kernel(tc, actions, W_ae, b_ae, ln_g, ln_b,
             nc.tensor.matmul(
                 out=neg_wbar_ps[:], lhsT=neg_mean_bf[:], rhs=w_nat[:, c, :], start=(c == 0), stop=(c == CHUNKS - 1)
             )
-        neg_b_ps = psum_y.tile([P, CHUNKS], F32, tag="y")
+        neg_b_ps = psum_t.tile([P, CHUNKS], F32, tag="t")
         nc.tensor.matmul(out=neg_b_ps[:], lhsT=neg_mean_f32[:], rhs=b_cols[:], start=True, stop=True)
         neg_w = const.tile([P, A], F32)
         nc.vector.tensor_copy(out=neg_w[:], in_=neg_wbar_ps[:])
@@ -352,25 +352,25 @@ def tile_actionbindingattention_pa_t_kernel(tc, actions, W_ae, b_ae, ln_g, ln_b,
                 project(slot - PROJECT_LAG)
             if slot < TILES:
                 encode(slot, 0)
-            ahead = slot + STATS_LEAD
-            if ahead < TILES and ahead % GROUP == 0:
-                statistics(ahead // GROUP)
             ahead = slot + DEVIATION_LEAD
             if ahead < TILES and ahead % GROUP == 0:
                 standard_deviation(ahead // GROUP)
             if slot < CHUNKS // 2:
                 prepare_wv(2 * slot)
                 prepare_wv(2 * slot + 1)
-            if slot in (2, 10, 18):
-                transpose_actions(slot + 6, slot + 14)
+            ahead = slot + STATS_LEAD
+            if ahead < TILES and ahead % GROUP == 0:
+                statistics(ahead // GROUP)
             behind = slot - TRANSPOSE_LAG
             if 0 <= behind < TILES:
                 transpose_pass(behind // GROUP, behind % GROUP)
-            behind = slot - REGROUP_LAG
-            if 0 <= behind < TILES:
-                regroup(behind // GROUP, behind % GROUP)
             behind = slot - QUANTISE_LAG
             if 0 <= behind < TILES:
                 quantise(behind // GROUP, behind % GROUP)
+            if slot in (2, 10, 18):
+                transpose_actions(slot + 6, slot + 14)
             if slot + BIAS_LEAD < TILES:
                 make_bias_row(slot + BIAS_LEAD)
+            behind = slot - REGROUP_LAG
+            if 0 <= behind < TILES:
+                regroup(behind // GROUP, behind % GROUP)

@@ -140,10 +140,6 @@ def tile_actionbindingattention_pa_t_kernel(tc, actions, W_ae, b_ae, ln_g, ln_b,
                 )
             nc.tensor.matmul(out=gram_ps[:, cols], lhsT=neg_w[:], rhs=neg_outer[:], start=False, stop=True)
         transpose_actions(0, GROUP)
-        wT = const.tile([P, F], BF16)
-        wT_ps = psum_o.tile([P, CHUNKS, P], BF16, tag="o")
-        for c in range(CHUNKS):
-            nc.tensor.transpose(wT_ps[:, c, :], w_nat[:, c, :], ident_bf[:])
         neg_c0_ps = psum_a.tile([P, CHUNKS], F32, tag="a")
         nc.tensor.matmul(out=neg_c0_ps[:], lhsT=neg_mean_f32[:], rhs=bc_sq[:], start=True, stop=True)
         stat_hi = const.tile([P, STAT_COLS], BF16)
@@ -156,7 +152,6 @@ def tile_actionbindingattention_pa_t_kernel(tc, actions, W_ae, b_ae, ln_g, ln_b,
         nc.vector.tensor_scalar(
             out=var_bias[:], in0=neg_var_b[:], scalar1=-1.0, scalar2=LN_EPS, op0=ALU.mult, op1=ALU.add
         )
-        nc.vector.tensor_copy(out=wT[:], in_=wT_ps[:].rearrange("p c f -> p (c f)"))
         bc_rows = const.tile([P, F], F32)
 
         def spread_bias():
@@ -245,7 +240,7 @@ def tile_actionbindingattention_pa_t_kernel(tc, actions, W_ae, b_ae, ln_g, ln_b,
             nc.vector.reciprocal(out=rstd_tile[:], in_=stds[group][:, r : r + 1])
             bias_tile = bias_pool.tile([P, F], F32)
             bias_rows[tile_i] = bias_tile
-            engine = nc.vector if group == 0 else nc.gpsimd
+            engine = nc.vector if tile_i == 0 else nc.gpsimd
             engine.tensor_scalar(
                 out=bias_tile[:],
                 in0=bc_rows[:],
@@ -297,10 +292,12 @@ def tile_actionbindingattention_pa_t_kernel(tc, actions, W_ae, b_ae, ln_g, ln_b,
         def regroup(group, g):
             grouped_tile = work.tile([P, GROUP_TOKENS, PACK], BF16, align_bytes=64)
             grouped[(group, g)] = grouped_tile
-            nc.vector.tensor_copy(
-                out=grouped_tile[:].rearrange("p (c i) j -> p c j i", i=4),
-                in_=planes[(group, g)][:].rearrange("p j (c i) -> p c j i", i=4),
-            )
+            grouped_view = grouped_tile[:].rearrange("p (c i) j -> p c j i", i=4)
+            planes_view = planes[(group, g)][:].rearrange("p j (c i) -> p c j i", i=4)
+            if g == 0 and GROUP * group + REGROUP_LAG <= PROJECT_LAG:
+                nc.scalar.copy(out=grouped_view, in_=planes_view)
+            else:
+                nc.vector.tensor_copy(out=grouped_view, in_=planes_view)
 
         def quantise(group, g):
             if g == 0:
@@ -335,10 +332,15 @@ def tile_actionbindingattention_pa_t_kernel(tc, actions, W_ae, b_ae, ln_g, ln_b,
                     nc.vector.tensor_copy(out=o_sb[:, cols], in_=o_ps[:])
                 else:
                     nc.scalar.copy(out=o_sb[:, cols], in_=o_ps[:])
-            nc.sync.dma_start(out=out_dram[:, tile_i, :], in_=o_sb[:])
+                nc.sync.dma_start(out=out_dram[:, tile_i, cols], in_=o_sb[:, cols])
 
+        wT = const.tile([P, F], BF16)
         spread_bias()
         statistics(0)
+        wT_ps = psum_o.tile([P, CHUNKS, P], BF16, tag="o")
+        for c in range(CHUNKS):
+            nc.tensor.transpose(wT_ps[:, c, :], w_nat[:, c, :], ident_bf[:])
+        nc.vector.tensor_copy(out=wT[:], in_=wT_ps[:].rearrange("p c f -> p (c f)"))
         standard_deviation(0)
         transpose_actions(GROUP, 8)
         make_bias_row(0)

@@ -55,9 +55,9 @@ def tile_actionbindingattention_pa_t_kernel(tc, actions, W_ae, b_ae, ln_g, ln_b,
         work = ctx.enter_context(tc.tile_pool(name="work", bufs=3))
         o_pool = ctx.enter_context(tc.tile_pool(name="o_pool", bufs=4))
         psum_y = ctx.enter_context(tc.psum_pool(name="psum_y", bufs=1))
-        psum_a = ctx.enter_context(tc.psum_pool(name="psum_a", bufs=2))
+        psum_a = ctx.enter_context(tc.psum_pool(name="psum_a", bufs=3))
         psum_t = ctx.enter_context(tc.psum_pool(name="psum_t", bufs=2))
-        psum_o = ctx.enter_context(tc.psum_pool(name="psum_o", bufs=3))
+        psum_o = ctx.enter_context(tc.psum_pool(name="psum_o", bufs=2))
 
         w_nat = const.tile([P, CHUNKS, A], BF16)
         nc.sync.dma_start(
@@ -294,7 +294,7 @@ def tile_actionbindingattention_pa_t_kernel(tc, actions, W_ae, b_ae, ln_g, ln_b,
             grouped[(group, g)] = grouped_tile
             grouped_view = grouped_tile[:].rearrange("p (c i) j -> p c j i", i=4)
             planes_view = planes[(group, g)][:].rearrange("p j (c i) -> p c j i", i=4)
-            if g == 0 and GROUP * group + REGROUP_LAG <= PROJECT_LAG:
+            if g == 0 and GROUP * group + REGROUP_LAG < PROJECT_LAG:
                 nc.scalar.copy(out=grouped_view, in_=planes_view)
             else:
                 nc.vector.tensor_copy(out=grouped_view, in_=planes_view)
@@ -369,8 +369,8 @@ def tile_actionbindingattention_pa_t_kernel(tc, actions, W_ae, b_ae, ln_g, ln_b,
             behind = slot - QUANTISE_LAG
             if 0 <= behind < TILES:
                 quantise(behind // GROUP, behind % GROUP)
-            if slot in (2, 10, 18):
-                transpose_actions(slot + 6, slot + 14)
+            if slot in (2, 3, 4):
+                transpose_actions(8 * slot - 8, 8 * slot)
             if slot + BIAS_LEAD < TILES:
                 make_bias_row(slot + BIAS_LEAD)
             behind = slot - REGROUP_LAG

@@ -292,12 +292,10 @@ def tile_actionbindingattention_pa_t_kernel(tc, actions, W_ae, b_ae, ln_g, ln_b,
         def regroup(group, g):
             grouped_tile = work.tile([P, GROUP_TOKENS, PACK], BF16, align_bytes=64)
             grouped[(group, g)] = grouped_tile
-            grouped_view = grouped_tile[:].rearrange("p (c i) j -> p c j i", i=4)
-            planes_view = planes[(group, g)][:].rearrange("p j (c i) -> p c j i", i=4)
-            if g == 0 and GROUP * group + REGROUP_LAG < PROJECT_LAG:
-                nc.scalar.copy(out=grouped_view, in_=planes_view)
-            else:
-                nc.vector.tensor_copy(out=grouped_view, in_=planes_view)
+            nc.vector.tensor_copy(
+                out=grouped_tile[:].rearrange("p (c i) j -> p c j i", i=4),
+                in_=planes[(group, g)][:].rearrange("p j (c i) -> p c j i", i=4),
+            )
 
         def quantise(group, g):
             if g == 0:
@@ -317,7 +315,10 @@ def tile_actionbindingattention_pa_t_kernel(tc, actions, W_ae, b_ae, ln_g, ln_b,
             o_sb = o_pool.tile([P, F], F32)
             for h in range(HALVES):
                 cols = slice(h * BANK, (h + 1) * BANK)
-                o_ps = psum_o.tile([P, BANK], F32, tag="o")
+                if tile_i + PROJECT_LAG >= TILES and h == 0:
+                    o_ps = psum_a.tile([P, BANK], F32, tag="a")
+                else:
+                    o_ps = psum_o.tile([P, BANK], F32, tag="o")
                 for g in range(PASSES):
                     nc.tensor.matmul_mx(
                         out=o_ps[:],
@@ -369,8 +370,8 @@ def tile_actionbindingattention_pa_t_kernel(tc, actions, W_ae, b_ae, ln_g, ln_b,
             behind = slot - QUANTISE_LAG
             if 0 <= behind < TILES:
                 quantise(behind // GROUP, behind % GROUP)
-            if slot in (2, 3, 4):
-                transpose_actions(8 * slot - 8, 8 * slot)
+            if slot in (3, 4, 5):
+                transpose_actions(8 * (slot - 2), 8 * (slot - 1))
             if slot + BIAS_LEAD < TILES:
                 make_bias_row(slot + BIAS_LEAD)
             behind = slot - REGROUP_LAG

@@ -171,8 +171,8 @@ def tile_actionbindingattention_pa_t_kernel(tc, actions, W_ae, b_ae, ln_g, ln_b,
         nc.vector.tensor_copy(out=shift_f[:], in_=s_bf[:].rearrange("p g t -> p (g t)"))
 
         wv_grouped = const.tile([P, PASSES, F, PACK], BF16, align_bytes=64)
-        wv_codes = const.tile([P, PASSES, F], U32, align_bytes=64)
-        wv_scales = const.tile([P, PASSES, F], U8, align_bytes=64)
+        wv_codes = const.tile([P, PASSES, F], U32, align_bytes=256)
+        wv_scales = const.tile([P, PASSES, F], U8, align_bytes=256)
 
         def prepare_wv(oc):
             words = wv_nat[:, oc, :].bitcast(F32)
@@ -299,8 +299,8 @@ def tile_actionbindingattention_pa_t_kernel(tc, actions, W_ae, b_ae, ln_g, ln_b,
 
         def quantise(group, g):
             if g == 0:
-                codes_tile = work.tile([P, PASSES, GROUP_TOKENS], U32, align_bytes=64)
-                scales_tile = work.tile([P, PASSES, GROUP_TOKENS], U8, align_bytes=64)
+                codes_tile = work.tile([P, PASSES, GROUP_TOKENS], U32, align_bytes=256)
+                scales_tile = work.tile([P, PASSES, GROUP_TOKENS], U8, align_bytes=256)
                 quantised[group] = (codes_tile, scales_tile)
             codes, scales = quantised[group]
             nc.vector.quantize_mx(

@@ -293,8 +293,8 @@ def tile_actionbindingattention_pa_t_kernel(tc, actions, W_ae, b_ae, ln_g, ln_b,
             grouped_tile = work.tile([P, GROUP_TOKENS, PACK], BF16, align_bytes=64)
             grouped[(group, g)] = grouped_tile
             nc.vector.tensor_copy(
-                out=grouped_tile[:].rearrange("p (c i) j -> p c j i", i=4),
-                in_=planes[(group, g)][:].rearrange("p j (c i) -> p c j i", i=4),
+                out=grouped_tile[:].rearrange("p (c i) j -> p c j i", i=8),
+                in_=planes[(group, g)][:].rearrange("p j (c i) -> p c j i", i=8),
             )
 
         def quantise(group, g):

@@ -186,15 +186,17 @@ def tile_actionbindingattention_pa_t_kernel(tc, actions, W_ae, b_ae, ln_g, ln_b,
                     .rearrange("p (o u) -> p o u", u=PACK // 2),
                     in_=wvT_ps[:, g, :, :].rearrange("p u o -> p o u"),
                 )
-            if (oc + 1) * P % BANK == 0:
-                cols = slice((oc + 1) * P - BANK, (oc + 1) * P)
-                for g in range(PASSES):
-                    nc.vector.quantize_mx(
-                        out=wv_codes[:, g, cols].bitcast(FP8X4),
-                        scales=wv_scales[:, g, cols],
-                        in_=wv_grouped[:, g, cols, :].rearrange("p o j -> p (o j)"),
-                    )
 
+        def quantise_wv(half):
+            cols = slice(half * BANK, (half + 1) * BANK)
+            for g in range(PASSES):
+                nc.vector.quantize_mx(
+                    out=wv_codes[:, g, cols].bitcast(FP8X4),
+                    scales=wv_scales[:, g, cols],
+                    in_=wv_grouped[:, g, cols, :].rearrange("p o j -> p (o j)"),
+                )
+
+        y_banks = {}
         f_vars = {}
         stds = {}
         rstd = {}
@@ -213,7 +215,7 @@ def tile_actionbindingattention_pa_t_kernel(tc, actions, W_ae, b_ae, ln_g, ln_b,
                 tile_i = group * GROUP + r
                 nc.tensor.matmul(out=y_ps[:, r, :], lhsT=xT[:, tile_i, :], rhs=stat_hi[:], start=True, stop=False)
                 nc.tensor.matmul(out=y_ps[:, r, :], lhsT=xT[:, tile_i, :], rhs=stat_lo[:], start=False, stop=True)
-            nc.scalar.copy(out=neg_mean[:], in_=y_ps[:, :, A + 1])
+            y_banks[group] = y_ps
             for r in range(GROUP):
                 products = work.tile([P, A + 1], F32)
                 nc.vector.scalar_tensor_tensor(
@@ -232,12 +234,14 @@ def tile_actionbindingattention_pa_t_kernel(tc, actions, W_ae, b_ae, ln_g, ln_b,
             std = stat_pool.tile([P, GROUP], F32)
             nc.scalar.activation(out=std[:], in_=f_vars[group][:], func=ACT.Sqrt, bias=var_bias[:], scale=1.0 / F)
             stds[group] = std
+            nc.scalar.copy(out=neg_means[group][:], in_=y_banks[group][:, :, A + 1])
 
         def make_bias_row(tile_i):
             group, r = divmod(tile_i, GROUP)
-            rstd_tile = stat_pool.tile([P, 1], F32)
-            rstd[tile_i] = rstd_tile
-            nc.vector.reciprocal(out=rstd_tile[:], in_=stds[group][:, r : r + 1])
+            if r == 0:
+                rstd_tile = stat_pool.tile([P, GROUP], F32)
+                rstd[group] = rstd_tile
+                nc.vector.reciprocal(out=rstd_tile[:], in_=stds[group][:])
             bias_tile = bias_pool.tile([P, F], F32)
             bias_rows[tile_i] = bias_tile
             engine = nc.vector if tile_i == 0 else nc.gpsimd
@@ -245,7 +249,7 @@ def tile_actionbindingattention_pa_t_kernel(tc, actions, W_ae, b_ae, ln_g, ln_b,
                 out=bias_tile[:],
                 in0=bc_rows[:],
                 scalar1=neg_means[group][:, r : r + 1],
-                scalar2=rstd_tile[:],
+                scalar2=rstd[group][:, r : r + 1],
                 op0=ALU.add,
                 op1=ALU.mult,
             )
@@ -260,7 +264,7 @@ def tile_actionbindingattention_pa_t_kernel(tc, actions, W_ae, b_ae, ln_g, ln_b,
             nc.vector.scalar_tensor_tensor(
                 out=n_tiles[tile_i][:, cols],
                 in0=a_ps[:],
-                scalar=rstd[tile_i][:],
+                scalar=rstd[tile_i // GROUP][:, tile_i % GROUP : tile_i % GROUP + 1],
                 in1=bias_rows[tile_i][:, cols],
                 op0=ALU.mult,
                 op1=ALU.add,
@@ -361,6 +365,8 @@ def tile_actionbindingattention_pa_t_kernel(tc, actions, W_ae, b_ae, ln_g, ln_b,
             if slot < CHUNKS // 2:
                 prepare_wv(2 * slot)
                 prepare_wv(2 * slot + 1)
+            if slot in (2, 4):
+                quantise_wv(slot // 2 - 1)
             ahead = slot + STATS_LEAD
             if ahead < TILES and ahead % GROUP == 0:
                 statistics(ahead // GROUP)

@@ -238,10 +238,9 @@ def tile_actionbindingattention_pa_t_kernel(tc, actions, W_ae, b_ae, ln_g, ln_b,
 
         def make_bias_row(tile_i):
             group, r = divmod(tile_i, GROUP)
-            if r == 0:
-                rstd_tile = stat_pool.tile([P, GROUP], F32)
-                rstd[group] = rstd_tile
-                nc.vector.reciprocal(out=rstd_tile[:], in_=stds[group][:])
+            rstd_tile = stat_pool.tile([P, 1], F32)
+            rstd[tile_i] = rstd_tile
+            nc.vector.reciprocal(out=rstd_tile[:], in_=stds[group][:, r : r + 1])
             bias_tile = bias_pool.tile([P, F], F32)
             bias_rows[tile_i] = bias_tile
             engine = nc.vector if tile_i == 0 else nc.gpsimd
@@ -249,7 +248,7 @@ def tile_actionbindingattention_pa_t_kernel(tc, actions, W_ae, b_ae, ln_g, ln_b,
                 out=bias_tile[:],
                 in0=bc_rows[:],
                 scalar1=neg_means[group][:, r : r + 1],
-                scalar2=rstd[group][:, r : r + 1],
+                scalar2=rstd_tile[:],
                 op0=ALU.add,
                 op1=ALU.mult,
             )
@@ -264,7 +263,7 @@ def tile_actionbindingattention_pa_t_kernel(tc, actions, W_ae, b_ae, ln_g, ln_b,
             nc.vector.scalar_tensor_tensor(
                 out=n_tiles[tile_i][:, cols],
                 in0=a_ps[:],
-                scalar=rstd[tile_i // GROUP][:, tile_i % GROUP : tile_i % GROUP + 1],
+                scalar=rstd[tile_i][:],
                 in1=bias_rows[tile_i][:, cols],
                 op0=ALU.mult,
                 op1=ALU.add,

@@ -37,6 +37,8 @@ TRANSPOSE_LAG = GROUP
 REGROUP_LAG = TRANSPOSE_LAG + 1
 QUANTISE_LAG = REGROUP_LAG + 1
 PROJECT_LAG = QUANTISE_LAG + 3
+WV_SLOTS = {0: (0, 1), 1: (2, 3), 2: (4, 5), 3: (6,), 4: (7,)}
+WV_QUANTISE = (2, 5)
 
 FLOPS = 2 * TOKENS * A * F + 2 * TOKENS * F * F
 
@@ -361,11 +363,10 @@ def tile_actionbindingattention_pa_t_kernel(tc, actions, W_ae, b_ae, ln_g, ln_b,
             ahead = slot + DEVIATION_LEAD
             if ahead < TILES and ahead % GROUP == 0:
                 standard_deviation(ahead // GROUP)
-            if slot < CHUNKS // 2:
-                prepare_wv(2 * slot)
-                prepare_wv(2 * slot + 1)
-            if slot in (2, 4):
-                quantise_wv(slot // 2 - 1)
+            for oc in WV_SLOTS.get(slot, ()):
+                prepare_wv(oc)
+            if slot in WV_QUANTISE:
+                quantise_wv(WV_QUANTISE.index(slot))
             ahead = slot + STATS_LEAD
             if ahead < TILES and ahead % GROUP == 0:
                 statistics(ahead // GROUP)
@@ -375,8 +376,9 @@ def tile_actionbindingattention_pa_t_kernel(tc, actions, W_ae, b_ae, ln_g, ln_b,
             behind = slot - QUANTISE_LAG
             if 0 <= behind < TILES:
                 quantise(behind // GROUP, behind % GROUP)
-            if slot in (3, 4, 5):
-                transpose_actions(8 * (slot - 2), 8 * (slot - 1))
+            if slot in (2, 4, 5):
+                first = 8 * max(1, slot - 2)
+                transpose_actions(first, first + 8)
             if slot + BIAS_LEAD < TILES:
                 make_bias_row(slot + BIAS_LEAD)
             behind = slot - REGROUP_LAG

from contextlib import ExitStack

import concourse.mybir as mybir
from concourse.masks import make_identity

F32 = mybir.dt.float32
BF16 = mybir.dt.bfloat16
U32 = mybir.dt.uint32
U8 = mybir.dt.uint8
FP8X4 = mybir.dt.float8_e4m3fn_x4
ALU = mybir.AluOpType
ACT = mybir.ActivationFunctionType
AXIS = mybir.AxisListType

P = 128
TOKENS = 32 * 128
A = 128
F = 1024
LN_EPS = 1e-5

TILES = TOKENS // P
GROUP = 2
GROUP_TOKENS = GROUP * P
CHUNKS = F // P
PACK = 4
PASSES = F // (P * PACK)
BANK = 512
HALVES = F // BANK
X_PITCH = A + 32
STAT_COLS = A + 2

STATS_LEAD = 4
WARM_UP = 12
DEVIATION_LEAD = 3
BIAS_LEAD = 2
TRANSPOSE_LAG = GROUP
REGROUP_LAG = TRANSPOSE_LAG + 1
QUANTISE_LAG = REGROUP_LAG + 1
PROJECT_LAG = QUANTISE_LAG + 3
WV_SLOTS = {0: (0, 1), 1: (2, 3), 2: (4, 5), 3: (6,), 4: (7,)}
WV_QUANTISE = (2, 5)

FLOPS = 2 * TOKENS * A * F + 2 * TOKENS * F * F


def tile_actionbindingattention_pa_t_kernel(tc, actions, W_ae, b_ae, ln_g, ln_b, Wv, out):
    nc = tc.nc
    x_dram = actions.rearrange("b n a -> (b n) a").rearrange("(p i) a -> p i a", i=TILES)
    out_dram = out.rearrange("b n o -> (b n) o").rearrange("(p i) o -> p i o", i=TILES)

    with ExitStack() as ctx:
        ctx.enter_context(tc.manual_schedule())
        const = ctx.enter_context(tc.tile_pool(name="const", bufs=1))
        stat_pool = ctx.enter_context(tc.tile_pool(name="stat_pool", bufs=STATS_LEAD))
        bias_pool = ctx.enter_context(tc.tile_pool(name="bias_pool", bufs=BIAS_LEAD + 2))
        n_pool = ctx.enter_context(tc.tile_pool(name="n_pool", bufs=8))
        work = ctx.enter_context(tc.tile_pool(name="work", bufs=3))
        o_pool = ctx.enter_context(tc.tile_pool(name="o_pool", bufs=4))
        psum_y = ctx.enter_context(tc.psum_pool(name="psum_y", bufs=1))
        psum_a = ctx.enter_context(tc.psum_pool(name="psum_a", bufs=3))
        psum_t = ctx.enter_context(tc.psum_pool(name="psum_t", bufs=2))
        psum_o = ctx.enter_context(tc.psum_pool(name="psum_o", bufs=2))

        w_nat = const.tile([P, CHUNKS, A], BF16)
        nc.sync.dma_start(
            out=w_nat[:].rearrange("p (g t) a -> p g (t a)", g=PASSES),
            in_=W_ae.rearrange("(g p t) a -> p g (t a)", g=PASSES, t=PACK),
        )
        g_bf = const.tile([P, PASSES, PACK], BF16)
        s_bf = const.tile([P, PASSES, PACK], BF16)
        b_bf = const.tile([P, PASSES, PACK], BF16)
        nc.sync.dma_start(out=b_bf[:], in_=b_ae.rearrange("(g p t) -> p g t", g=PASSES, t=PACK))
        x_aug = const.tile([P, TILES, X_PITCH], BF16)

        def load_actions(first, end):
            nc.sync.dma_start(out=x_aug[:, first:end, 0:A], in_=x_dram[:, first:end, :])

        load_actions(0, GROUP)
        for cols_bf, vec in ((g_bf, ln_g), (s_bf, ln_b)):
            nc.sync.dma_start(out=cols_bf[:], in_=vec.rearrange("(g p t) -> p g t", g=PASSES, t=PACK))
        load_actions(GROUP, 8)
        wv_nat = const.tile([P, CHUNKS, F], BF16)
        wv_dram = Wv.rearrange("(oc p) k -> p oc k", p=P)
        for q in range(4):
            nc.sync.dma_start(out=wv_nat[:, 2 * q : 2 * q + 2, :], in_=wv_dram[:, 2 * q : 2 * q + 2, :])
            if q in (0, 1, 3):
                load_actions({0: 8, 1: 16, 3: 24}[q], {0: 16, 1: 24, 3: 32}[q])

        neg_mean_bf = const.tile([P, P], BF16)
        nc.vector.memset(neg_mean_bf[:], -1.0 / F)
        neg_mean_f32 = const.tile([P, P], F32)
        nc.vector.memset(neg_mean_f32[:], -1.0 / F)
        side = const.tile([P, CHUNKS, 2], BF16)
        nc.vector.memset(side[:], -1.0 / F)
        neg_b8 = const.tile([P, 2], F32)
        nc.vector.memset(neg_b8[:], 0.0)
        warm = const.tile([P, 1], F32)
        nc.scalar.activation(out=warm[:], in_=neg_mean_f32[:, 0:1], func=ACT.Sqrt, scale=-1.0)
        ident_bf = const.tile([P, P], BF16)
        make_identity(nc, ident_bf[:])
        ident_f32 = const.tile([P, P], F32)
        make_identity(nc, ident_f32[:])
        nc.vector.memset(x_aug[:, :, A : A + 1], 2.0)
        warm_ps = psum_t.tile([P, P], F32, tag="t")
        for i in range(WARM_UP):
            nc.tensor.matmul(out=warm_ps[:], lhsT=neg_mean_bf[:], rhs=neg_mean_bf[:], start=True, stop=True)

        b_cols = const.tile([P, CHUNKS], F32)
        nc.vector.tensor_copy(out=b_cols[:], in_=b_bf[:].rearrange("p g t -> p (g t)"))
        nc.vector.tensor_copy(out=side[:, :, 0], in_=b_bf[:].rearrange("p g t -> p (g t)"))
        neg_wbar_ps = psum_y.tile([P, A], F32, tag="y")
        for c in range(CHUNKS):
            nc.tensor.matmul(
                out=neg_wbar_ps[:], lhsT=neg_mean_bf[:], rhs=w_nat[:, c, :], start=(c == 0), stop=(c == CHUNKS - 1)
            )
        neg_b_ps = psum_t.tile([P, CHUNKS], F32, tag="t")
        nc.tensor.matmul(out=neg_b_ps[:], lhsT=neg_mean_f32[:], rhs=b_cols[:], start=True, stop=True)
        neg_w = const.tile([P, A], F32)
        nc.vector.tensor_copy(out=neg_w[:], in_=neg_wbar_ps[:])
        w8 = const.tile([P, A], F32)
        nc.vector.tensor_scalar(out=w8[:], in0=neg_wbar_ps[:], scalar1=-F / P, scalar2=None, op0=ALU.mult)
        neg_bbar = const.tile([P, 1], F32)
        nc.vector.tensor_reduce(out=neg_bbar[:], in_=neg_b_ps[:], axis=AXIS.X, op=ALU.add)
        nc.vector.tensor_scalar(out=neg_b8[:, 0:1], in0=neg_bbar[:], scalar1=-F / P, scalar2=None, op0=ALU.mult)
        bc_cols = const.tile([P, CHUNKS], F32)
        nc.vector.tensor_scalar(out=bc_cols[:], in0=b_cols[:], scalar1=neg_bbar[:], scalar2=None, op0=ALU.add)
        bc_sq = const.tile([P, CHUNKS], F32)
        nc.vector.tensor_tensor(out=bc_sq[:], in0=bc_cols[:], in1=bc_cols[:], op=ALU.mult)
        xT = const.tile([P, TILES, P], BF16)

        def transpose_actions(first, end):
            xT_ps = psum_o.tile([P, CHUNKS, P], BF16, tag="o")
            for i in range(first, end):
                nc.tensor.transpose(xT_ps[:, i - first, :], x_aug[:, i, 0:A], ident_bf[:])
            nc.scalar.copy(out=xT[:, first:end, :], in_=xT_ps[:, 0 : end - first, :])

        gram_ps = psum_a.tile([P, STAT_COLS], F32, tag="a")
        for cols, moving, neg_outer in ((slice(0, A), w_nat, w8), (slice(A, STAT_COLS), side, neg_b8)):
            for c in range(CHUNKS):
                nc.tensor.matmul(
                    out=gram_ps[:, cols], lhsT=w_nat[:, c, :], rhs=moving[:, c, :], start=(c == 0), stop=False
                )
            nc.tensor.matmul(out=gram_ps[:, cols], lhsT=neg_w[:], rhs=neg_outer[:], start=False, stop=True)
        transpose_actions(0, GROUP)
        neg_c0_ps = psum_a.tile([P, CHUNKS], F32, tag="a")
        nc.tensor.matmul(out=neg_c0_ps[:], lhsT=neg_mean_f32[:], rhs=bc_sq[:], start=True, stop=True)
        stat_hi = const.tile([P, STAT_COLS], BF16)
        nc.vector.tensor_copy(out=stat_hi[:], in_=gram_ps[:])
        stat_lo = const.tile([P, STAT_COLS], BF16)
        nc.vector.tensor_tensor(out=stat_lo[:], in0=gram_ps[:], in1=stat_hi[:], op=ALU.subtract)
        neg_var_b = const.tile([P, 1], F32)
        nc.vector.tensor_reduce(out=neg_var_b[:], in_=neg_c0_ps[:], axis=AXIS.X, op=ALU.add)
        var_bias = const.tile([P, 1], F32)
        nc.vector.tensor_scalar(
            out=var_bias[:], in0=neg_var_b[:], scalar1=-1.0, scalar2=LN_EPS, op0=ALU.mult, op1=ALU.add
        )
        bc_rows = const.tile([P, F], F32)

        def spread_bias():
            for half in range(2):
                bc_ps = psum_t.tile([P, BANK], F32, tag="t")
                for c in range(CHUNKS // 2):
                    nc.tensor.transpose(
                        bc_ps[:, c * P : (c + 1) * P],
                        bc_cols[:, half * CHUNKS // 2 + c : half * CHUNKS // 2 + c + 1].to_broadcast([P, P]),
                        ident_f32[:],
                    )
                nc.scalar.copy(out=bc_rows[:, half * BANK : (half + 1) * BANK], in_=bc_ps[:])

        gain = const.tile([P, CHUNKS], F32)
        nc.vector.tensor_copy(out=gain[:], in_=g_bf[:].rearrange("p g t -> p (g t)"))
        shift_f = const.tile([P, CHUNKS], F32)
        nc.vector.tensor_copy(out=shift_f[:], in_=s_bf[:].rearrange("p g t -> p (g t)"))

        wv_grouped = const.tile([P, PASSES, F, PACK], BF16, align_bytes=64)
        wv_codes = const.tile([P, PASSES, F], U32, align_bytes=256)
        wv_scales = const.tile([P, PASSES, F], U8, align_bytes=256)

        def prepare_wv(oc):
            words = wv_nat[:, oc, :].bitcast(F32)
            wvT_ps = psum_o.tile([P, PASSES, PACK // 2, P], F32, tag="o")
            for g in range(PASSES):
                for u in range(PACK // 2):
                    nc.tensor.transpose(wvT_ps[:, g, u, :], words[:, 2 * P * g + u : 2 * P * (g + 1) : 2], ident_f32[:])
            for g in range(PASSES):
                nc.scalar.copy(
                    out=wv_grouped[:, g, oc * P : (oc + 1) * P, :].rearrange("p o j -> p (o j)").bitcast(F32)
                    .rearrange("p (o u) -> p o u", u=PACK // 2),
                    in_=wvT_ps[:, g, :, :].rearrange("p u o -> p o u"),
                )

        def quantise_wv(half):
            cols = slice(half * BANK, (half + 1) * BANK)
            for g in range(PASSES):
                nc.vector.quantize_mx(
                    out=wv_codes[:, g, cols].bitcast(FP8X4),
                    scales=wv_scales[:, g, cols],
                    in_=wv_grouped[:, g, cols, :].rearrange("p o j -> p (o j)"),
                )

        y_banks = {}
        f_vars = {}
        stds = {}
        rstd = {}
        neg_means = {}
        bias_rows = {}
        n_tiles = {}
        planes = {}
        grouped = {}
        quantised = {}

        def statistics(group):
            f_var = stat_pool.tile([P, GROUP], F32)
            neg_mean = stat_pool.tile([P, GROUP], F32)
            y_ps = psum_y.tile([P, GROUP, STAT_COLS], F32, tag="y")
            for r in range(GROUP):
                tile_i = group * GROUP + r
                nc.tensor.matmul(out=y_ps[:, r, :], lhsT=xT[:, tile_i, :], rhs=stat_hi[:], start=True, stop=False)
                nc.tensor.matmul(out=y_ps[:, r, :], lhsT=xT[:, tile_i, :], rhs=stat_lo[:], start=False, stop=True)
            y_banks[group] = y_ps
            for r in range(GROUP):
                products = work.tile([P, A + 1], F32)
                nc.vector.scalar_tensor_tensor(
                    out=products[:],
                    in0=y_ps[:, r, 0 : A + 1],
                    scalar=1.0,
                    in1=x_aug[:, group * GROUP + r, 0 : A + 1],
                    op0=ALU.mult,
                    op1=ALU.mult,
                    accum_out=f_var[:, r : r + 1],
                )
            f_vars[group] = f_var
            neg_means[group] = neg_mean

        def standard_deviation(group):
            std = stat_pool.tile([P, GROUP], F32)
            nc.scalar.activation(out=std[:], in_=f_vars[group][:], func=ACT.Sqrt, bias=var_bias[:], scale=1.0 / F)
            stds[group] = std
            nc.scalar.copy(out=neg_means[group][:], in_=y_banks[group][:, :, A + 1])

        def make_bias_row(tile_i):
            group, r = divmod(tile_i, GROUP)
            rstd_tile = stat_pool.tile([P, 1], F32)
            rstd[tile_i] = rstd_tile
            nc.vector.reciprocal(out=rstd_tile[:], in_=stds[group][:, r : r + 1])
            bias_tile = bias_pool.tile([P, F], F32)
            bias_rows[tile_i] = bias_tile
            engine = nc.vector if tile_i == 0 else nc.gpsimd
            engine.tensor_scalar(
                out=bias_tile[:],
                in0=bc_rows[:],
                scalar1=neg_means[group][:, r : r + 1],
                scalar2=rstd_tile[:],
                op0=ALU.add,
                op1=ALU.mult,
            )

        def encode(tile_i, h):
            if h == 0:
                n_sb = n_pool.tile([P, F], F32)
                n_tiles[tile_i] = n_sb
            cols = slice(h * BANK, (h + 1) * BANK)
            a_ps = psum_a.tile([P, BANK], F32, tag="a")
            nc.tensor.matmul(out=a_ps[:], lhsT=xT[:, tile_i, :], rhs=wT[:, cols], start=True, stop=True)
            nc.vector.scalar_tensor_tensor(
                out=n_tiles[tile_i][:, cols],
                in0=a_ps[:],
                scalar=rstd[tile_i][:],
                in1=bias_rows[tile_i][:, cols],
                op0=ALU.mult,
                op1=ALU.add,
            )

        def transpose_pass(group, g):
            planes_tile = work.tile([P, PACK, GROUP_TOKENS], BF16)
            planes[(group, g)] = planes_tile
            for t0 in range(0, PACK, 2):
                t_ps = psum_t.tile([P, 2, GROUP_TOKENS], F32, tag="t")
                for e in range(2):
                    c = g * PACK + t0 + e
                    for r in range(GROUP):
                        nc.tensor.transpose(
                            t_ps[:, e, r * P : (r + 1) * P],
                            n_tiles[group * GROUP + r][:, c * P : (c + 1) * P],
                            ident_f32[:],
                        )
                for e in range(2):
                    c = g * PACK + t0 + e
                    nc.scalar.activation(
                        out=planes_tile[:, t0 + e, :],
                        in_=t_ps[:, e, :],
                        func=ACT.Identity,
                        scale=gain[:, c : c + 1],
                        bias=shift_f[:, c : c + 1],
                    )

        def regroup(group, g):
            grouped_tile = work.tile([P, GROUP_TOKENS, PACK], BF16, align_bytes=64)
            grouped[(group, g)] = grouped_tile
            nc.vector.tensor_copy(
                out=grouped_tile[:].rearrange("p (c i) j -> p c j i", i=8),
                in_=planes[(group, g)][:].rearrange("p j (c i) -> p c j i", i=8),
            )

        def quantise(group, g):
            if g == 0:
                codes_tile = work.tile([P, PASSES, GROUP_TOKENS], U32, align_bytes=256)
                scales_tile = work.tile([P, PASSES, GROUP_TOKENS], U8, align_bytes=256)
                quantised[group] = (codes_tile, scales_tile)
            codes, scales = quantised[group]
            nc.vector.quantize_mx(
                out=codes[:, g, :].bitcast(FP8X4),
                scales=scales[:, g, :],
                in_=grouped[(group, g)][:].rearrange("p w j -> p (w j)"),
            )

        def project(tile_i):
            codes, scales = quantised[tile_i // GROUP]
            tokens = slice(tile_i % GROUP * P, (tile_i % GROUP + 1) * P)
            o_sb = o_pool.tile([P, F], F32)
            for h in range(HALVES):
                cols = slice(h * BANK, (h + 1) * BANK)
                if tile_i + PROJECT_LAG >= TILES and h == 0:
                    o_ps = psum_a.tile([P, BANK], F32, tag="a")
                else:
                    o_ps = psum_o.tile([P, BANK], F32, tag="o")
                for g in range(PASSES):
                    nc.tensor.matmul_mx(
                        out=o_ps[:],
                        lhsT=codes[:, g, tokens].bitcast(FP8X4),
                        lhsT_scale=scales[:, g, tokens],
                        rhs=wv_codes[:, g, cols].bitcast(FP8X4),
                        rhs_scale=wv_scales[:, g, cols],
                        start=(g == 0),
                        stop=(g == PASSES - 1),
                    )
                if tile_i + PROJECT_LAG >= TILES and h == 1:
                    nc.vector.tensor_copy(out=o_sb[:, cols], in_=o_ps[:])
                else:
                    nc.scalar.copy(out=o_sb[:, cols], in_=o_ps[:])
                nc.sync.dma_start(out=out_dram[:, tile_i, cols], in_=o_sb[:, cols])

        wT = const.tile([P, F], BF16)
        spread_bias()
        statistics(0)
        wT_ps = psum_o.tile([P, CHUNKS, P], BF16, tag="o")
        for c in range(CHUNKS):
            nc.tensor.transpose(wT_ps[:, c, :], w_nat[:, c, :], ident_bf[:])
        nc.vector.tensor_copy(out=wT[:], in_=wT_ps[:].rearrange("p c f -> p (c f)"))
        standard_deviation(0)
        transpose_actions(GROUP, 8)
        make_bias_row(0)
        make_bias_row(1)
        statistics(1)
        standard_deviation(1)
        for slot in range(TILES + PROJECT_LAG):
            if 0 <= slot - 1 < TILES:
                encode(slot - 1, 1)
            if 0 <= slot - PROJECT_LAG:
                project(slot - PROJECT_LAG)
            if slot < TILES:
                encode(slot, 0)
            ahead = slot + DEVIATION_LEAD
            if ahead < TILES and ahead % GROUP == 0:
                standard_deviation(ahead // GROUP)
            for oc in WV_SLOTS.get(slot, ()):
                prepare_wv(oc)
            if slot in WV_QUANTISE:
                quantise_wv(WV_QUANTISE.index(slot))
            ahead = slot + STATS_LEAD
            if ahead < TILES and ahead % GROUP == 0:
                statistics(ahead // GROUP)
            behind = slot - TRANSPOSE_LAG
            if 0 <= behind < TILES:
                transpose_pass(behind // GROUP, behind % GROUP)
            behind = slot - QUANTISE_LAG
            if 0 <= behind < TILES:
                quantise(behind // GROUP, behind % GROUP)
            if slot in (2, 4, 5):
                first = 8 * max(1, slot - 2)
                transpose_actions(first, first + 8)
            if slot + BIAS_LEAD < TILES:
                make_bias_row(slot + BIAS_LEAD)
            behind = slot - REGROUP_LAG
            if 0 <= behind < TILES:
                regroup(behind // GROUP, behind % GROUP)
